import numpy as np
import ml_dtypes


def mxq(x, axis, fmt="e4m3"):
    dtype, down = {"e4m3": (ml_dtypes.float8_e4m3fn, 7), "e5m2": (ml_dtypes.float8_e5m2, 14)}[fmt]
    v = np.moveaxis(np.asarray(x, np.float32).astype(ml_dtypes.bfloat16).astype(np.float64), axis, -1)
    blocks = v.reshape(v.shape[:-1] + (-1, 32))
    amax = np.abs(blocks).max(-1, keepdims=True)
    byte = np.maximum(np.where(amax > 0, np.frexp(amax)[1] - 1 + 127, 0) - down, 1)
    scale = np.exp2(byte - 127.0)
    codes = (blocks / scale).astype(np.float32).astype(dtype).astype(np.float64)
    return np.moveaxis((codes * scale).reshape(v.shape), -1, axis)


WIDE = False


def mx_kscale(k):
    if not WIDE:
        return np.ones(k)
    levels = np.array([30, -30])
    if k % 512:
        return np.exp2(np.random.permutation(np.resize(levels, k // 32))).repeat(32)
    a = np.empty((k // 512, 16))
    for p in range(k // 512):
        a[p, :8] = np.random.permutation(np.resize(levels, 8))
        for g in range(8):
            far = levels[np.abs(levels - a[p, g]) >= 10]
            a[p, g + 8] = far[np.random.randint(len(far))]
    return np.exp2(a.ravel()).repeat(32)


BF16 = ml_dtypes.bfloat16


def bf(x):
    return np.asarray(x, np.float32).astype(BF16)


def f64(x):
    return np.asarray(x).astype(np.float64)


B, S, D, NH, NKV, HD, QB = 1, 512, 2048, 16, 4, 128, 512
Q_DIM = NH * HD
KV_DIM = NKV * HD


def rot(t, f0, f1):
    tp = t.reshape(t.shape[:-1] + (HD // 2, 2))
    t0, t1 = tp[..., 0], tp[..., 1]
    row1 = t0 * f0 + t1 * f1
    row0 = t0 * f1 - t1 * f0
    return np.stack([row0, row1], axis=-1).reshape(t.shape)


def setup_inputs():
    s = mx_kscale(D)
    return {"x": bf(np.random.standard_normal((B, S, D)) * s),
            "freqs_cis": bf(np.random.standard_normal((S, HD))),
            "Wqkv": bf(np.random.standard_normal((Q_DIM + 2 * KV_DIM, D)) / np.sqrt(D) / s)}


def reference(x, freqs_cis, Wqkv):
    xqkv = mxq(f64(x), 2, "e5m2") @ mxq(f64(Wqkv), 1, "e5m2").T
    xq = xqkv[..., :Q_DIM].reshape(B, S, NH, HD)
    xk = xqkv[..., Q_DIM:Q_DIM + KV_DIM].reshape(B, S, NKV, HD)
    xv = xqkv[..., Q_DIM + KV_DIM:].reshape(B, S, NKV, HD)
    f = f64(freqs_cis).reshape(S, 1, HD // 2, 2)
    f0, f1 = f[..., 0], f[..., 1]
    q_rot = rot(xq, f0, f1).transpose(0, 2, 1, 3)
    k_rot = rot(xk, f0, f1).transpose(0, 2, 1, 3)
    v = xv.transpose(0, 2, 1, 3)
    return q_rot, k_rot, v

@@ -1,0 +1,226 @@
+from contextlib import ExitStack
+
+import concourse.mybir as mybir
+from concourse.masks import make_identity
+
+F32 = mybir.dt.float32
+BF16 = mybir.dt.bfloat16
+U32 = mybir.dt.uint32
+U8 = mybir.dt.uint8
+E5X4 = mybir.dt.float8_e5m2_x4
+MULT = mybir.AluOpType.mult
+ADD = mybir.AluOpType.add
+
+P = 128
+HD = 128
+K_PASS = 512
+PASSES = 4
+W_GROUPS = 6
+FLOPS = 2 * 512 * 2048 * 3072
+
+ADD_ON_POOL = False
+EARLY_GROUPS = 4
+
+
+def tile_rlaattention_pa_kernel(tc, x, freqs_cis, Wqkv, out_0, out_1, out_2):
+    nc = tc.nc
+    with ExitStack() as ctx:
+        const = ctx.enter_context(tc.tile_pool(name="const", bufs=1))
+        raw = ctx.enter_context(tc.tile_pool(name="raw", bufs=1))
+        grp_pool = ctx.enter_context(tc.tile_pool(name="grp", bufs=6))
+        code_pool = ctx.enter_context(tc.tile_pool(name="code", bufs=12))
+        work = ctx.enter_context(tc.tile_pool(name="work", bufs=3))
+        tp_pool = ctx.enter_context(tc.psum_pool(name="tp", bufs=4))
+        acc_pool = ctx.enter_context(tc.psum_pool(name="acc", bufs=4))
+        ctx.enter_context(tc.manual_schedule())
+
+        f_sb = const.tile([P, 4, HD], BF16, name="f_sb")
+        nc.scalar.dma_start(out=f_sb[:], in_=freqs_cis.rearrange("(p m) d -> p m d", m=4))
+        x_view = x.flatten_outer_dims().rearrange("(p m) k -> p m k", m=4)
+        source = {}
+
+        def rows_of(grp):
+            if grp == 0:
+                return x_view
+            return Wqkv[(grp - 1) * 512 : grp * 512, :].rearrange("(j p) k -> p j k", p=P)
+
+        def load_pass(grp, g):
+            t = raw.tile([P, 4, K_PASS], BF16, name="rawk%d_%d" % (grp, g))
+            nc.sync.dma_start(out=t[:], in_=rows_of(grp)[:, :, K_PASS * g : K_PASS * (g + 1)])
+            for j in range(4):
+                source[(grp, g, j)] = (t, j, 0)
+
+        def load_rows(grp, rp):
+            t = raw.tile([P, 2, K_PASS * PASSES], BF16, name="rawr%d_%d" % (grp, rp))
+            nc.sync.dma_start(out=t[:], in_=rows_of(grp)[:, 2 * rp : 2 * rp + 2, :])
+            for g in range(PASSES):
+                for jj in range(2):
+                    source[(grp, g, 2 * rp + jj)] = (t, jj, 256 * g)
+
+        for g in range(PASSES):
+            load_pass(0, g)
+            load_pass(1, g)
+        for grp in range(2, EARLY_GROUPS + 1):
+            load_rows(grp, 0)
+            load_rows(grp, 1)
+        late_loads = [(grp, rp) for grp in range(EARLY_GROUPS + 1, W_GROUPS + 1) for rp in range(2)]
+
+        ident = const.tile([P, P], F32, name="ident")
+        make_identity(nc, ident[:])
+        warm = const.tile([P, 1], F32, name="warm")
+        nc.scalar.copy(out=warm[:], in_=ident[:, 0:1])
+
+        tab_a = const.tile([P, 4, HD], F32, name="tab_a")
+        tab_b = const.tile([P, 4, HD], F32, name="tab_b")
+        f_pairs = f_sb[:].rearrange("p m (j e) -> p m j e", e=2)
+        a_pairs = tab_a[:].rearrange("p m (j e) -> p m j e", e=2)
+        b_pairs = tab_b[:].rearrange("p m (j e) -> p m j e", e=2)
+        nc.vector.tensor_copy(out=a_pairs[:, :, :, 0], in_=f_pairs[:, :, :, 1])
+        nc.vector.tensor_copy(out=a_pairs[:, :, :, 1], in_=f_pairs[:, :, :, 1])
+        nc.vector.tensor_copy(out=b_pairs[:, :, :, 0], in_=f_pairs[:, :, :, 0])
+        nc.vector.tensor_scalar_mul(out=b_pairs[:, :, :, 1], in0=f_pairs[:, :, :, 0], scalar1=-1.0)
+
+        grouped = {}
+        codes = {}
+        scales = {}
+        acc = {}
+        prod = {}
+        res = {}
+
+        def transposes(grp, g):
+            gt = grp_pool.tile([P, 4 * 512], BF16, name="gt", align_bytes=64)
+            gw = gt[:].bitcast(F32).rearrange("p (r u) -> p r u", u=2)
+            for rp in range(2):
+                bank = tp_pool.tile([P, 512], F32, name="bank")
+                for u in range(2):
+                    for jj in range(2):
+                        t, j, w0 = source[(grp, g, 2 * rp + jj)]
+                        words = t[:, j, :].bitcast(F32)
+                        c0 = 256 * u + 128 * jj
+                        nc.tensor.transpose(bank[:, c0 : c0 + 128], words[:, w0 + u : w0 + 256 : 2], ident[:])
+                nc.scalar.copy(
+                    out=gw[:, 256 * rp : 256 * (rp + 1), :],
+                    in_=bank[:].rearrange("p (u r) -> p r u", u=2),
+                )
+            grouped[(grp, g)] = gt
+
+        def quantize(grp, g):
+            if grp == 0:
+                c = const.tile([P, 512], U32, name="xc%d" % g, align_bytes=64)
+                s = const.tile([P, 512], U8, name="xs%d" % g, align_bytes=64)
+            else:
+                c = code_pool.tile([P, 512], U32, name="wc", align_bytes=64)
+                s = code_pool.tile([P, 512], U8, name="ws", align_bytes=64)
+            nc.vector.quantize_mx(out=c[:].bitcast(E5X4), scales=s[:], in_=grouped[(grp, g)][:])
+            codes[(grp, g)] = c
+            scales[(grp, g)] = s
+
+        def mx(n, m, g):
+            if g == 0:
+                acc[(n, m)] = acc_pool.tile([P, 512], F32, name="acc")
+            cols = slice(128 * m, 128 * (m + 1))
+            nc.tensor.matmul_mx(
+                out=acc[(n, m)][:],
+                lhsT=codes[(0, g)][:, cols].bitcast(E5X4),
+                lhsT_scale=scales[(0, g)][:, cols],
+                rhs=codes[(n + 1, g)][:].bitcast(E5X4),
+                rhs_scale=scales[(n + 1, g)][:],
+                start=(g == 0),
+                stop=(g == PASSES - 1),
+            )
+
+        def result_tile(n, m):
+            if m % 2 == 0:
+                res[(n, m // 2)] = work.tile([P, 4, 2, HD], F32, name="res")
+            return res[(n, m // 2)][:, :, m % 2, :]
+
+        def rope_products(n, m):
+            a3 = acc[(n, m)][:].rearrange("p (h c) -> p h c", h=4)
+            m1 = work.tile([P, 4, HD], F32, name="m1")
+            m2 = work.tile([P, 4, HD], F32, name="m2")
+            nc.vector.tensor_tensor(out=m1[:], in0=a3, in1=tab_a[:, m : m + 1, :].to_broadcast([P, 4, HD]), op=MULT)
+            nc.vector.tensor_tensor(out=m2[:], in0=a3, in1=tab_b[:, m : m + 1, :].to_broadcast([P, 4, HD]), op=MULT)
+            prod[(n, m)] = (m1, m2)
+
+        def rope_add(n, m):
+            m1, m2 = prod[(n, m)]
+            eng = nc.gpsimd if ADD_ON_POOL else nc.vector
+            eng.tensor_tensor(
+                out=result_tile(n, m).rearrange("p h (j e) -> p h j e", e=2),
+                in0=m1[:].rearrange("p h (j e) -> p h j e", e=2),
+                in1=m2[:].rearrange("p h (j e) -> p h j e", e=2)[:, :, :, ::-1],
+                op=ADD,
+            )
+            if m % 2 == 1:
+                store(n, m // 2)
+
+        def plain_copy(n, m):
+            nc.scalar.copy(out=result_tile(n, m), in_=acc[(n, m)][:].rearrange("p (h c) -> p h c", h=4))
+            if m % 2 == 1:
+                store(n, m // 2)
+
+        def store(n, mp):
+            if n < 4:
+                dst = out_0[0, 4 * n : 4 * n + 4]
+            elif n == 4:
+                dst = out_1[0]
+            else:
+                dst = out_2[0]
+            view = dst.rearrange("h (p a b) d -> p a h (b d)", a=2, b=2)
+            nc.sync.dma_start(out=view[:, mp], in_=res[(n, mp)][:].rearrange("p h b d -> p h (b d)"))
+            if len(late_loads) > 0:
+                grp, rp = late_loads[0]
+                late_loads.remove((grp, rp))
+                load_rows(grp, rp)
+
+        for g in range(2):
+            transposes(0, g)
+            transposes(1, g)
+        for g in range(2):
+            quantize(0, g)
+            quantize(1, g)
+        for g in range(PASSES):
+            for m in range(4):
+                mx(0, m, g)
+            if g < 2:
+                transposes(0, g + 2)
+                transposes(1, g + 2)
+                quantize(0, g + 2)
+                quantize(1, g + 2)
+            elif g == 2:
+                transposes(2, 0)
+                transposes(2, 1)
+                quantize(2, 0)
+                quantize(2, 1)
+        transposes(2, 2)
+        transposes(2, 3)
+        transposes(3, 0)
+        transposes(3, 1)
+        for m in range(4):
+            rope_products(0, m)
+            if m < 2:
+                quantize(2, 2 + m)
+            rope_add(0, m)
+
+        for n in range(1, W_GROUPS):
+            for half in range(2):
+                ms = (2 * half, 2 * half + 1)
+                for m in ms:
+                    for g in range(PASSES):
+                        mx(n, m, g)
+                late = n + 2 == W_GROUPS and half == 1
+                if late:
+                    quantize(n + 2, 2)
+                    quantize(n + 2, 3)
+                for m in ms:
+                    if n == W_GROUPS - 1:
+                        plain_copy(n, m)
+                    else:
+                        rope_products(n, m)
+                        if n + 2 <= W_GROUPS and not late:
+                            quantize(n + 2, m)
+                        rope_add(n, m)
+                nxt = (n + 2, 2) if half == 0 else (n + 3, 0)
+                if nxt[0] <= W_GROUPS:
+                    transposes(nxt[0], nxt[1])
+                    transposes(nxt[0], nxt[1] + 1)

@@ -18,8 +18,232 @@ PASSES = 4
 W_GROUPS = 6
 FLOPS = 2 * 512 * 2048 * 3072
 
-ADD_ON_POOL = False
-EARLY_GROUPS = 4
+ADD_ON_POOL = True
+SINGLE_FROM = 4
+CODE_BUFS = 12
+REORDERED = ()
+
+LOADS = (
+    ("k", 0, 0, 1),
+    ("k", 1, 0, 1),
+    ("k", 0, 1, 1),
+    ("k", 1, 1, 1),
+    ("f", 0, 0, 0),
+    ("k", 0, 2, 1),
+    ("k", 1, 2, 1),
+    ("k", 0, 3, 1),
+    ("k", 1, 3, 1),
+    ("k", 2, 0, 2),
+    ("k", 2, 2, 2),
+    ("k", 3, 0, 2),
+    ("k", 3, 2, 2),
+    ("k", 4, 0, 2),
+    ("k", 4, 2, 2),
+)
+
+PROGRAM = (
+    ("T", 0, 0),
+    ("T", 1, 0),
+    ("T", 0, 1),
+    ("T", 1, 1),
+    ("Q", 0, 0),
+    ("Q", 1, 0),
+    ("Q", 0, 1),
+    ("Q", 1, 1),
+    ("B"),
+    ("M", 0, 0, 0),
+    ("M", 0, 1, 0),
+    ("M", 0, 2, 0),
+    ("M", 0, 3, 0),
+    ("T", 0, 2),
+    ("T", 1, 2),
+    ("Q", 0, 2),
+    ("Q", 1, 2),
+    ("M", 0, 0, 1),
+    ("M", 0, 1, 1),
+    ("M", 0, 2, 1),
+    ("M", 0, 3, 1),
+    ("T", 0, 3),
+    ("T", 1, 3),
+    ("Q", 0, 3),
+    ("Q", 1, 3),
+    ("M", 0, 0, 2),
+    ("M", 0, 1, 2),
+    ("M", 0, 2, 2),
+    ("M", 0, 3, 2),
+    ("T", 2, 0),
+    ("T", 2, 1),
+    ("Q", 2, 0),
+    ("Q", 2, 1),
+    ("M", 0, 0, 3),
+    ("M", 0, 1, 3),
+    ("M", 0, 2, 3),
+    ("M", 0, 3, 3),
+    ("T", 2, 2),
+    ("T", 2, 3),
+    ("T", 3, 0),
+    ("T", 3, 1),
+    ("R", 0, 0),
+    ("Q", 2, 2),
+    ("A", 0, 0),
+    ("R", 0, 1),
+    ("Q", 2, 3),
+    ("A", 0, 1),
+    ("L", 5, 0, 2),
+    ("R", 0, 2),
+    ("A", 0, 2),
+    ("R", 0, 3),
+    ("A", 0, 3),
+    ("L", 5, 2, 2),
+    ("M", 1, 0, 0),
+    ("M", 1, 0, 1),
+    ("M", 1, 0, 2),
+    ("M", 1, 0, 3),
+    ("M", 1, 1, 0),
+    ("M", 1, 1, 1),
+    ("M", 1, 1, 2),
+    ("M", 1, 1, 3),
+    ("R", 1, 0),
+    ("Q", 3, 0),
+    ("A", 1, 0),
+    ("R", 1, 1),
+    ("Q", 3, 1),
+    ("A", 1, 1),
+    ("L", 6, 0, 2),
+    ("T", 3, 2),
+    ("T", 3, 3),
+    ("M", 1, 2, 0),
+    ("M", 1, 2, 1),
+    ("M", 1, 2, 2),
+    ("M", 1, 2, 3),
+    ("M", 1, 3, 0),
+    ("M", 1, 3, 1),
+    ("M", 1, 3, 2),
+    ("M", 1, 3, 3),
+    ("R", 1, 2),
+    ("Q", 3, 2),
+    ("A", 1, 2),
+    ("R", 1, 3),
+    ("Q", 3, 3),
+    ("A", 1, 3),
+    ("L", 6, 2, 2),
+    ("T", 4, 0),
+    ("T", 4, 1),
+    ("M", 2, 0, 0),
+    ("M", 2, 0, 1),
+    ("M", 2, 0, 2),
+    ("M", 2, 0, 3),
+    ("M", 2, 1, 0),
+    ("M", 2, 1, 1),
+    ("M", 2, 1, 2),
+    ("M", 2, 1, 3),
+    ("R", 2, 0),
+    ("Q", 4, 0),
+    ("A", 2, 0),
+    ("R", 2, 1),
+    ("Q", 4, 1),
+    ("A", 2, 1),
+    ("T", 4, 2),
+    ("T", 4, 3),
+    ("M", 2, 2, 0),
+    ("M", 2, 2, 1),
+    ("M", 2, 2, 2),
+    ("M", 2, 2, 3),
+    ("M", 2, 3, 0),
+    ("M", 2, 3, 1),
+    ("M", 2, 3, 2),
+    ("M", 2, 3, 3),
+    ("R", 2, 2),
+    ("Q", 4, 2),
+    ("A", 2, 2),
+    ("R", 2, 3),
+    ("Q", 4, 3),
+    ("A", 2, 3),
+    ("T", 5, 0),
+    ("T", 5, 1),
+    ("M", 3, 0, 0),
+    ("M", 3, 0, 1),
+    ("M", 3, 0, 2),
+    ("M", 3, 0, 3),
+    ("M", 3, 1, 0),
+    ("M", 3, 1, 1),
+    ("M", 3, 1, 2),
+    ("M", 3, 1, 3),
+    ("R", 3, 0),
+    ("Q", 5, 0),
+    ("A", 3, 0),
+    ("R", 3, 1),
+    ("Q", 5, 1),
+    ("A", 3, 1),
+    ("T", 5, 2),
+    ("T", 5, 3),
+    ("M", 3, 2, 0),
+    ("M", 3, 2, 1),
+    ("M", 3, 2, 2),
+    ("M", 3, 2, 3),
+    ("M", 3, 3, 0),
+    ("M", 3, 3, 1),
+    ("M", 3, 3, 2),
+    ("M", 3, 3, 3),
+    ("R", 3, 2),
+    ("Q", 5, 2),
+    ("A", 3, 2),
+    ("R", 3, 3),
+    ("Q", 5, 3),
+    ("A", 3, 3),
+    ("T", 6, 0),
+    ("T", 6, 1),
+    ("T", 6, 2),
+    ("T", 6, 3),
+    ("Q", 6, 0),
+    ("Q", 6, 1),
+    ("Q", 6, 2),
+    ("Q", 6, 3),
+    ("M", 4, 0, 0),
+    ("M", 4, 0, 1),
+    ("M", 4, 0, 2),
+    ("M", 4, 0, 3),
+    ("M", 4, 1, 0),
+    ("M", 4, 1, 1),
+    ("M", 4, 1, 2),
+    ("M", 4, 1, 3),
+    ("R", 4, 0),
+    ("A", 4, 0),
+    ("R", 4, 1),
+    ("A", 4, 1),
+    ("M", 5, 0, 0),
+    ("M", 5, 0, 1),
+    ("M", 5, 0, 2),
+    ("M", 5, 0, 3),
+    ("M", 5, 1, 0),
+    ("M", 5, 1, 1),
+    ("M", 5, 1, 2),
+    ("M", 5, 1, 3),
+    ("C", 5, 0),
+    ("C", 5, 1),
+    ("M", 4, 2, 0),
+    ("M", 4, 2, 1),
+    ("M", 4, 2, 2),
+    ("M", 4, 2, 3),
+    ("M", 4, 3, 0),
+    ("M", 4, 3, 1),
+    ("M", 4, 3, 2),
+    ("M", 4, 3, 3),
+    ("R", 4, 2),
+    ("A", 4, 2),
+    ("R", 4, 3),
+    ("A", 4, 3),
+    ("M", 5, 2, 0),
+    ("M", 5, 2, 1),
+    ("M", 5, 2, 2),
+    ("M", 5, 2, 3),
+    ("M", 5, 3, 0),
+    ("M", 5, 3, 1),
+    ("M", 5, 3, 2),
+    ("M", 5, 3, 3),
+    ("C", 5, 2),
+    ("C", 5, 3),
+)
 
 
 def tile_rlaattention_pa_kernel(tc, x, freqs_cis, Wqkv, out_0, out_1, out_2):
@@ -28,42 +252,36 @@ def tile_rlaattention_pa_kernel(tc, x, freqs_cis, Wqkv, out_0, out_1, out_2):
         const = ctx.enter_context(tc.tile_pool(name="const", bufs=1))
         raw = ctx.enter_context(tc.tile_pool(name="raw", bufs=1))
         grp_pool = ctx.enter_context(tc.tile_pool(name="grp", bufs=6))
-        code_pool = ctx.enter_context(tc.tile_pool(name="code", bufs=12))
+        code_pool = ctx.enter_context(tc.tile_pool(name="code", bufs=CODE_BUFS))
         work = ctx.enter_context(tc.tile_pool(name="work", bufs=3))
         tp_pool = ctx.enter_context(tc.psum_pool(name="tp", bufs=4))
         acc_pool = ctx.enter_context(tc.psum_pool(name="acc", bufs=4))
         ctx.enter_context(tc.manual_schedule())
 
-        f_sb = const.tile([P, 4, HD], BF16, name="f_sb")
-        nc.scalar.dma_start(out=f_sb[:], in_=freqs_cis.rearrange("(p m) d -> p m d", m=4))
         x_view = x.flatten_outer_dims().rearrange("(p m) k -> p m k", m=4)
         source = {}
+        f_sb = const.tile([P, 4, HD], BF16, name="f_sb")
 
         def rows_of(grp):
             if grp == 0:
                 return x_view
             return Wqkv[(grp - 1) * 512 : grp * 512, :].rearrange("(j p) k -> p j k", p=P)
 
-        def load_pass(grp, g):
-            t = raw.tile([P, 4, K_PASS], BF16, name="rawk%d_%d" % (grp, g))
-            nc.sync.dma_start(out=t[:], in_=rows_of(grp)[:, :, K_PASS * g : K_PASS * (g + 1)])
-            for j in range(4):
-                source[(grp, g, j)] = (t, j, 0)
+        def load_passes(grp, g0, count):
+            t = raw.tile([P, 4, K_PASS * count], BF16, name="rawk%d_%d" % (grp, g0))
+            nc.sync.dma_start(out=t[:], in_=rows_of(grp)[:, :, K_PASS * g0 : K_PASS * (g0 + count)])
+            for g in range(g0, g0 + count):
+                for j in range(4):
+                    source[(grp, g, j)] = (t, j, 256 * (g - g0), 2)
 
-        def load_rows(grp, rp):
-            t = raw.tile([P, 2, K_PASS * PASSES], BF16, name="rawr%d_%d" % (grp, rp))
-            nc.sync.dma_start(out=t[:], in_=rows_of(grp)[:, 2 * rp : 2 * rp + 2, :])
-            for g in range(PASSES):
-                for jj in range(2):
-                    source[(grp, g, 2 * rp + jj)] = (t, jj, 256 * g)
+        def load(entry):
+            if entry[0] == "f":
+                nc.sync.dma_start(out=f_sb[:], in_=freqs_cis.rearrange("(p m) d -> p m d", m=4))
+            else:
+                load_passes(entry[1], entry[2], entry[3])
 
-        for g in range(PASSES):
-            load_pass(0, g)
-            load_pass(1, g)
-        for grp in range(2, EARLY_GROUPS + 1):
-            load_rows(grp, 0)
-            load_rows(grp, 1)
-        late_loads = [(grp, rp) for grp in range(EARLY_GROUPS + 1, W_GROUPS + 1) for rp in range(2)]
+        for entry in LOADS:
+            load(entry)
 
         ident = const.tile([P, P], F32, name="ident")
         make_identity(nc, ident[:])
@@ -72,13 +290,15 @@ def tile_rlaattention_pa_kernel(tc, x, freqs_cis, Wqkv, out_0, out_1, out_2):
 
         tab_a = const.tile([P, 4, HD], F32, name="tab_a")
         tab_b = const.tile([P, 4, HD], F32, name="tab_b")
-        f_pairs = f_sb[:].rearrange("p m (j e) -> p m j e", e=2)
-        a_pairs = tab_a[:].rearrange("p m (j e) -> p m j e", e=2)
-        b_pairs = tab_b[:].rearrange("p m (j e) -> p m j e", e=2)
-        nc.vector.tensor_copy(out=a_pairs[:, :, :, 0], in_=f_pairs[:, :, :, 1])
-        nc.vector.tensor_copy(out=a_pairs[:, :, :, 1], in_=f_pairs[:, :, :, 1])
-        nc.vector.tensor_copy(out=b_pairs[:, :, :, 0], in_=f_pairs[:, :, :, 0])
-        nc.vector.tensor_scalar_mul(out=b_pairs[:, :, :, 1], in0=f_pairs[:, :, :, 0], scalar1=-1.0)
+
+        def build_tables():
+            f_pairs = f_sb[:].rearrange("p m (j e) -> p m j e", e=2)
+            a_pairs = tab_a[:].rearrange("p m (j e) -> p m j e", e=2)
+            b_pairs = tab_b[:].rearrange("p m (j e) -> p m j e", e=2)
+            nc.vector.tensor_copy(out=a_pairs[:, :, :, 0], in_=f_pairs[:, :, :, 1])
+            nc.vector.tensor_copy(out=a_pairs[:, :, :, 1], in_=f_pairs[:, :, :, 1])
+            nc.vector.tensor_copy(out=b_pairs[:, :, :, 0], in_=f_pairs[:, :, :, 0])
+            nc.vector.tensor_scalar_mul(out=b_pairs[:, :, :, 1], in0=f_pairs[:, :, :, 0], scalar1=-1.0)
 
         grouped = {}
         codes = {}
@@ -87,6 +307,14 @@ def tile_rlaattention_pa_kernel(tc, x, freqs_cis, Wqkv, out_0, out_1, out_2):
         prod = {}
         res = {}
 
+        def reorder(grp, gp, j):
+            t, jj, w0, step = source[(grp, 2 * gp, j)]
+            ro = work.tile([P, 2, 2, 128], F32, name="ro", bufs=6)
+            words = t[:, jj, :].bitcast(F32)[:, w0 : w0 + 512]
+            nc.scalar.copy(out=ro[:], in_=words.rearrange("r (g p u) -> r g u p", g=2, u=2))
+            for gg in range(2):
+                source[(grp, 2 * gp + gg, j)] = (ro, gg, 0, 1)
+
         def transposes(grp, g):
             gt = grp_pool.tile([P, 4 * 512], BF16, name="gt", align_bytes=64)
             gw = gt[:].bitcast(F32).rearrange("p (r u) -> p r u", u=2)
@@ -94,10 +322,13 @@ def tile_rlaattention_pa_kernel(tc, x, freqs_cis, Wqkv, out_0, out_1, out_2):
                 bank = tp_pool.tile([P, 512], F32, name="bank")
                 for u in range(2):
                     for jj in range(2):
-                        t, j, w0 = source[(grp, g, 2 * rp + jj)]
-                        words = t[:, j, :].bitcast(F32)
+                        t, j, w0, step = source[(grp, g, 2 * rp + jj)]
                         c0 = 256 * u + 128 * jj
-                        nc.tensor.transpose(bank[:, c0 : c0 + 128], words[:, w0 + u : w0 + 256 : 2], ident[:])
+                        if step == 2:
+                            words = t[:, j, :].bitcast(F32)[:, w0 + u : w0 + 256 : 2]
+                        else:
+                            words = t[:, j, u, :]
+                        nc.tensor.transpose(bank[:, c0 : c0 + 128], words, ident[:])
                 nc.scalar.copy(
                     out=gw[:, 256 * rp : 256 * (rp + 1), :],
                     in_=bank[:].rearrange("p (u r) -> p r u", u=2),
@@ -130,6 +361,9 @@ def tile_rlaattention_pa_kernel(tc, x, freqs_cis, Wqkv, out_0, out_1, out_2):
             )
 
         def result_tile(n, m):
+            if n >= SINGLE_FROM:
+                res[(n, m)] = work.tile([P, 4, HD], F32, name="res1", bufs=8)
+                return res[(n, m)][:]
             if m % 2 == 0:
                 res[(n, m // 2)] = work.tile([P, 4, 2, HD], F32, name="res")
             return res[(n, m // 2)][:, :, m % 2, :]
@@ -151,76 +385,43 @@ def tile_rlaattention_pa_kernel(tc, x, freqs_cis, Wqkv, out_0, out_1, out_2):
                 in1=m2[:].rearrange("p h (j e) -> p h j e", e=2)[:, :, :, ::-1],
                 op=ADD,
             )
-            if m % 2 == 1:
-                store(n, m // 2)
+            store(nc.sync, n, m)
 
         def plain_copy(n, m):
             nc.scalar.copy(out=result_tile(n, m), in_=acc[(n, m)][:].rearrange("p (h c) -> p h c", h=4))
-            if m % 2 == 1:
-                store(n, m // 2)
+            store(nc.scalar, n, m)
 
-        def store(n, mp):
+        def store(queue, n, m):
             if n < 4:
                 dst = out_0[0, 4 * n : 4 * n + 4]
             elif n == 4:
                 dst = out_1[0]
             else:
                 dst = out_2[0]
-            view = dst.rearrange("h (p a b) d -> p a h (b d)", a=2, b=2)
-            nc.sync.dma_start(out=view[:, mp], in_=res[(n, mp)][:].rearrange("p h b d -> p h (b d)"))
-            if len(late_loads) > 0:
-                grp, rp = late_loads[0]
-                late_loads.remove((grp, rp))
-                load_rows(grp, rp)
+            if n >= SINGLE_FROM:
+                view = dst.rearrange("h (p m) d -> p m h d", m=4)
+                queue.dma_start(out=view[:, m], in_=res[(n, m)][:])
+            elif m % 2 == 1:
+                view = dst.rearrange("h (p a b) d -> p a h (b d)", a=2, b=2)
+                queue.dma_start(out=view[:, m // 2], in_=res[(n, m // 2)][:].rearrange("p h b d -> p h (b d)"))
 
-        for g in range(2):
-            transposes(0, g)
-            transposes(1, g)
-        for g in range(2):
-            quantize(0, g)
-            quantize(1, g)
-        for g in range(PASSES):
-            for m in range(4):
-                mx(0, m, g)
-            if g < 2:
-                transposes(0, g + 2)
-                transposes(1, g + 2)
-                quantize(0, g + 2)
-                quantize(1, g + 2)
-            elif g == 2:
-                transposes(2, 0)
-                transposes(2, 1)
-                quantize(2, 0)
-                quantize(2, 1)
-        transposes(2, 2)
-        transposes(2, 3)
-        transposes(3, 0)
-        transposes(3, 1)
-        for m in range(4):
-            rope_products(0, m)
-            if m < 2:
-                quantize(2, 2 + m)
-            rope_add(0, m)
-
-        for n in range(1, W_GROUPS):
-            for half in range(2):
-                ms = (2 * half, 2 * half + 1)
-                for m in ms:
-                    for g in range(PASSES):
-                        mx(n, m, g)
-                late = n + 2 == W_GROUPS and half == 1
-                if late:
-                    quantize(n + 2, 2)
-                    quantize(n + 2, 3)
-                for m in ms:
-                    if n == W_GROUPS - 1:
-                        plain_copy(n, m)
-                    else:
-                        rope_products(n, m)
-                        if n + 2 <= W_GROUPS and not late:
-                            quantize(n + 2, m)
-                        rope_add(n, m)
-                nxt = (n + 2, 2) if half == 0 else (n + 3, 0)
-                if nxt[0] <= W_GROUPS:
-                    transposes(nxt[0], nxt[1])
-                    transposes(nxt[0], nxt[1] + 1)
+        for step in PROGRAM:
+            kind = step[0]
+            if kind == "T":
+                transposes(step[1], step[2])
+            elif kind == "Q":
+                quantize(step[1], step[2])
+            elif kind == "M":
+                mx(step[1], step[2], step[3])
+            elif kind == "R":
+                rope_products(step[1], step[2])
+            elif kind == "A":
+                rope_add(step[1], step[2])
+            elif kind == "C":
+                plain_copy(step[1], step[2])
+            elif kind == "L":
+                load_passes(step[1], step[2], step[3])
+            elif kind == "O":
+                reorder(step[1], step[2], step[3])
+            else:
+                build_tables()

@@ -24,15 +24,15 @@ CODE_BUFS = 12
 REORDERED = ()
 
 LOADS = (
-    ("k", 0, 0, 1),
+    ("x", 0, 0, 0),
     ("k", 1, 0, 1),
-    ("k", 0, 1, 1),
     ("k", 1, 1, 1),
-    ("f", 0, 0, 0),
-    ("k", 0, 2, 1),
     ("k", 1, 2, 1),
-    ("k", 0, 3, 1),
     ("k", 1, 3, 1),
+    ("x", 1, 0, 0),
+    ("f", 0, 0, 0),
+    ("x", 2, 0, 0),
+    ("x", 3, 0, 0),
     ("k", 2, 0, 2),
     ("k", 2, 2, 2),
     ("k", 3, 0, 2),
@@ -42,58 +42,70 @@ LOADS = (
 )
 
 PROGRAM = (
-    ("T", 0, 0),
+    ("W", 6),
+    ("TX", 0),
+    ("W", 1),
+    ("QX", 0),
     ("T", 1, 0),
-    ("T", 0, 1),
-    ("T", 1, 1),
-    ("Q", 0, 0),
+    ("W", 1),
     ("Q", 1, 0),
-    ("Q", 0, 1),
+    ("T", 1, 1),
+    ("W", 1),
     ("Q", 1, 1),
+    ("T", 1, 2),
+    ("W", 1),
+    ("Q", 1, 2),
+    ("T", 1, 3),
+    ("W", 1),
+    ("Q", 1, 3),
+    ("TX", 1),
+    ("QX", 1),
     ("B"),
     ("M", 0, 0, 0),
-    ("M", 0, 1, 0),
-    ("M", 0, 2, 0),
-    ("M", 0, 3, 0),
-    ("T", 0, 2),
-    ("T", 1, 2),
-    ("Q", 0, 2),
-    ("Q", 1, 2),
     ("M", 0, 0, 1),
-    ("M", 0, 1, 1),
-    ("M", 0, 2, 1),
-    ("M", 0, 3, 1),
-    ("T", 0, 3),
-    ("T", 1, 3),
-    ("Q", 0, 3),
-    ("Q", 1, 3),
     ("M", 0, 0, 2),
+    ("M", 0, 0, 3),
+    ("TX", 2),
+    ("TX", 3),
+    ("R", 0, 0),
+    ("A", 0, 0),
+    ("QX", 2),
+    ("QX", 3),
+    ("M", 0, 1, 0),
+    ("M", 0, 1, 1),
     ("M", 0, 1, 2),
-    ("M", 0, 2, 2),
-    ("M", 0, 3, 2),
+    ("M", 0, 1, 3),
     ("T", 2, 0),
     ("T", 2, 1),
+    ("R", 0, 1),
     ("Q", 2, 0),
+    ("A", 0, 1),
     ("Q", 2, 1),
-    ("M", 0, 0, 3),
-    ("M", 0, 1, 3),
+    ("L", 5, 0, 2),
+    ("M", 0, 2, 0),
+    ("M", 0, 2, 1),
+    ("M", 0, 2, 2),
     ("M", 0, 2, 3),
-    ("M", 0, 3, 3),
+    ("O", 3, 0, 0),
+    ("O", 3, 0, 1),
     ("T", 2, 2),
     ("T", 2, 3),
+    ("R", 0, 2),
+    ("Q", 2, 2),
+    ("A", 0, 2),
+    ("Q", 2, 3),
+    ("M", 0, 3, 0),
+    ("M", 0, 3, 1),
+    ("M", 0, 3, 2),
+    ("M", 0, 3, 3),
+    ("O", 3, 1, 0),
+    ("O", 3, 1, 1),
     ("T", 3, 0),
     ("T", 3, 1),
-    ("R", 0, 0),
-    ("Q", 2, 2),
-    ("A", 0, 0),
-    ("R", 0, 1),
-    ("Q", 2, 3),
-    ("A", 0, 1),
-    ("L", 5, 0, 2),
-    ("R", 0, 2),
-    ("A", 0, 2),
     ("R", 0, 3),
+    ("Q", 3, 0),
     ("A", 0, 3),
+    ("Q", 3, 1),
     ("L", 5, 2, 2),
     ("M", 1, 0, 0),
     ("M", 1, 0, 1),
@@ -103,15 +115,17 @@ PROGRAM = (
     ("M", 1, 1, 1),
     ("M", 1, 1, 2),
     ("M", 1, 1, 3),
-    ("R", 1, 0),
-    ("Q", 3, 0),
-    ("A", 1, 0),
-    ("R", 1, 1),
-    ("Q", 3, 1),
-    ("A", 1, 1),
-    ("L", 6, 0, 2),
+    ("O", 4, 0, 0),
+    ("O", 4, 0, 1),
     ("T", 3, 2),
     ("T", 3, 3),
+    ("R", 1, 0),
+    ("Q", 3, 2),
+    ("A", 1, 0),
+    ("R", 1, 1),
+    ("Q", 3, 3),
+    ("A", 1, 1),
+    ("L", 6, 0, 2),
     ("M", 1, 2, 0),
     ("M", 1, 2, 1),
     ("M", 1, 2, 2),
@@ -120,15 +134,17 @@ PROGRAM = (
     ("M", 1, 3, 1),
     ("M", 1, 3, 2),
     ("M", 1, 3, 3),
-    ("R", 1, 2),
-    ("Q", 3, 2),
-    ("A", 1, 2),
-    ("R", 1, 3),
-    ("Q", 3, 3),
-    ("A", 1, 3),
-    ("L", 6, 2, 2),
+    ("O", 4, 1, 0),
+    ("O", 4, 1, 1),
     ("T", 4, 0),
     ("T", 4, 1),
+    ("R", 1, 2),
+    ("Q", 4, 0),
+    ("A", 1, 2),
+    ("R", 1, 3),
+    ("Q", 4, 1),
+    ("A", 1, 3),
+    ("L", 6, 2, 2),
     ("M", 2, 0, 0),
     ("M", 2, 0, 1),
     ("M", 2, 0, 2),
@@ -137,14 +153,16 @@ PROGRAM = (
     ("M", 2, 1, 1),
     ("M", 2, 1, 2),
     ("M", 2, 1, 3),
-    ("R", 2, 0),
-    ("Q", 4, 0),
-    ("A", 2, 0),
-    ("R", 2, 1),
-    ("Q", 4, 1),
-    ("A", 2, 1),
+    ("O", 5, 0, 0),
+    ("O", 5, 0, 1),
     ("T", 4, 2),
     ("T", 4, 3),
+    ("R", 2, 0),
+    ("Q", 4, 2),
+    ("A", 2, 0),
+    ("R", 2, 1),
+    ("Q", 4, 3),
+    ("A", 2, 1),
     ("M", 2, 2, 0),
     ("M", 2, 2, 1),
     ("M", 2, 2, 2),
@@ -153,14 +171,16 @@ PROGRAM = (
     ("M", 2, 3, 1),
     ("M", 2, 3, 2),
     ("M", 2, 3, 3),
-    ("R", 2, 2),
-    ("Q", 4, 2),
-    ("A", 2, 2),
-    ("R", 2, 3),
-    ("Q", 4, 3),
-    ("A", 2, 3),
+    ("O", 5, 1, 0),
+    ("O", 5, 1, 1),
     ("T", 5, 0),
     ("T", 5, 1),
+    ("R", 2, 2),
+    ("Q", 5, 0),
+    ("A", 2, 2),
+    ("R", 2, 3),
+    ("Q", 5, 1),
+    ("A", 2, 3),
     ("M", 3, 0, 0),
     ("M", 3, 0, 1),
     ("M", 3, 0, 2),
@@ -169,14 +189,16 @@ PROGRAM = (
     ("M", 3, 1, 1),
     ("M", 3, 1, 2),
     ("M", 3, 1, 3),
-    ("R", 3, 0),
-    ("Q", 5, 0),
-    ("A", 3, 0),
-    ("R", 3, 1),
-    ("Q", 5, 1),
-    ("A", 3, 1),
+    ("O", 6, 0, 0),
+    ("O", 6, 0, 1),
     ("T", 5, 2),
     ("T", 5, 3),
+    ("R", 3, 0),
+    ("Q", 5, 2),
+    ("A", 3, 0),
+    ("R", 3, 1),
+    ("Q", 5, 3),
+    ("A", 3, 1),
     ("M", 3, 2, 0),
     ("M", 3, 2, 1),
     ("M", 3, 2, 2),
@@ -185,20 +207,16 @@ PROGRAM = (
     ("M", 3, 3, 1),
     ("M", 3, 3, 2),
     ("M", 3, 3, 3),
-    ("R", 3, 2),
-    ("Q", 5, 2),
-    ("A", 3, 2),
-    ("R", 3, 3),
-    ("Q", 5, 3),
-    ("A", 3, 3),
+    ("O", 6, 1, 0),
+    ("O", 6, 1, 1),
     ("T", 6, 0),
     ("T", 6, 1),
-    ("T", 6, 2),
-    ("T", 6, 3),
+    ("R", 3, 2),
     ("Q", 6, 0),
+    ("A", 3, 2),
+    ("R", 3, 3),
     ("Q", 6, 1),
-    ("Q", 6, 2),
-    ("Q", 6, 3),
+    ("A", 3, 3),
     ("M", 4, 0, 0),
     ("M", 4, 0, 1),
     ("M", 4, 0, 2),
@@ -207,32 +225,35 @@ PROGRAM = (
     ("M", 4, 1, 1),
     ("M", 4, 1, 2),
     ("M", 4, 1, 3),
+    ("T", 6, 2),
+    ("T", 6, 3),
     ("R", 4, 0),
+    ("Q", 6, 2),
     ("A", 4, 0),
     ("R", 4, 1),
+    ("Q", 6, 3),
     ("A", 4, 1),
-    ("M", 5, 0, 0),
-    ("M", 5, 0, 1),
-    ("M", 5, 0, 2),
-    ("M", 5, 0, 3),
-    ("M", 5, 1, 0),
-    ("M", 5, 1, 1),
-    ("M", 5, 1, 2),
-    ("M", 5, 1, 3),
-    ("C", 5, 0),
-    ("C", 5, 1),
     ("M", 4, 2, 0),
     ("M", 4, 2, 1),
     ("M", 4, 2, 2),
     ("M", 4, 2, 3),
+    ("R", 4, 2),
+    ("A", 4, 2),
+    ("M", 5, 0, 0),
+    ("M", 5, 0, 1),
+    ("M", 5, 0, 2),
+    ("M", 5, 0, 3),
+    ("C", 5, 0),
     ("M", 4, 3, 0),
     ("M", 4, 3, 1),
     ("M", 4, 3, 2),
     ("M", 4, 3, 3),
-    ("R", 4, 2),
-    ("A", 4, 2),
     ("R", 4, 3),
     ("A", 4, 3),
+    ("M", 5, 1, 0),
+    ("M", 5, 1, 1),
+    ("M", 5, 1, 2),
+    ("M", 5, 1, 3),
     ("M", 5, 2, 0),
     ("M", 5, 2, 1),
     ("M", 5, 2, 2),
@@ -241,6 +262,7 @@ PROGRAM = (
     ("M", 5, 3, 1),
     ("M", 5, 3, 2),
     ("M", 5, 3, 3),
+    ("C", 5, 1),
     ("C", 5, 2),
     ("C", 5, 3),
 )
@@ -251,7 +273,7 @@ def tile_rlaattention_pa_kernel(tc, x, freqs_cis, Wqkv, out_0, out_1, out_2):
     with ExitStack() as ctx:
         const = ctx.enter_context(tc.tile_pool(name="const", bufs=1))
         raw = ctx.enter_context(tc.tile_pool(name="raw", bufs=1))
-        grp_pool = ctx.enter_context(tc.tile_pool(name="grp", bufs=6))
+        grp_pool = ctx.enter_context(tc.tile_pool(name="grp", bufs=5))
         code_pool = ctx.enter_context(tc.tile_pool(name="code", bufs=CODE_BUFS))
         work = ctx.enter_context(tc.tile_pool(name="work", bufs=3))
         tp_pool = ctx.enter_context(tc.psum_pool(name="tp", bufs=4))
@@ -274,8 +296,15 @@ def tile_rlaattention_pa_kernel(tc, x, freqs_cis, Wqkv, out_0, out_1, out_2):
                 for j in range(4):
                     source[(grp, g, j)] = (t, j, 256 * (g - g0), 2)
 
+        def load_x(m):
+            t = raw.tile([P, K_PASS * PASSES], BF16, name="rawx%d" % m)
+            nc.sync.dma_start(out=t[:], in_=x_view[:, m, :])
+            source[("x", m)] = t
+
         def load(entry):
-            if entry[0] == "f":
+            if entry[0] == "x":
+                load_x(entry[1])
+            elif entry[0] == "f":
                 nc.sync.dma_start(out=f_sb[:], in_=freqs_cis.rearrange("(p m) d -> p m d", m=4))
             else:
                 load_passes(entry[1], entry[2], entry[3])
@@ -287,6 +316,16 @@ def tile_rlaattention_pa_kernel(tc, x, freqs_cis, Wqkv, out_0, out_1, out_2):
         make_identity(nc, ident[:])
         warm = const.tile([P, 1], F32, name="warm")
         nc.scalar.copy(out=warm[:], in_=ident[:, 0:1])
+
+        zeros = const.tile([P, 512], BF16, name="zeros")
+        nc.vector.memset(zeros[:], 0.0)
+        idle = {}
+
+        def keep_warm(count):
+            if len(idle) == 0:
+                idle[0] = acc_pool.tile([P, 512], F32, name="acc")
+            for i in range(count):
+                nc.tensor.matmul(out=idle[0][:], lhsT=zeros[:, 0:P], rhs=zeros[:], start=True, stop=True)
 
         tab_a = const.tile([P, 4, HD], F32, name="tab_a")
         tab_b = const.tile([P, 4, HD], F32, name="tab_b")
@@ -335,13 +374,37 @@ def tile_rlaattention_pa_kernel(tc, x, freqs_cis, Wqkv, out_0, out_1, out_2):
                 )
             grouped[(grp, g)] = gt
 
+        def transposes_x(m):
+            words = source[("x", m)][:].bitcast(F32)
+            gt = grp_pool.tile([P, 4 * 512], BF16, name="gt", align_bytes=64)
+            gw = gt[:].bitcast(F32).rearrange("p (g r u) -> p g r u", g=PASSES, u=2)
+            for gp in range(2):
+                bank = tp_pool.tile([P, 512], F32, name="bank")
+                for gg in range(2):
+                    for u in range(2):
+                        g = 2 * gp + gg
+                        c0 = 256 * gg + 128 * u
+                        nc.tensor.transpose(bank[:, c0 : c0 + 128], words[:, 256 * g + u : 256 * (g + 1) : 2], ident[:])
+                nc.scalar.copy(
+                    out=gw[:, 2 * gp : 2 * gp + 2, :, :],
+                    in_=bank[:].rearrange("p (g u r) -> p g r u", g=2, u=2),
+                )
+            grouped[("x", m)] = gt
+
+        def quantize_x(m):
+            c = const.tile([P, PASSES, P], U32, name="xc%d" % m, align_bytes=64)
+            s = const.tile([P, PASSES, P], U8, name="xs%d" % m, align_bytes=64)
+            nc.vector.quantize_mx(
+                out=c[:].rearrange("p g r -> p (g r)").bitcast(E5X4),
+                scales=s[:].rearrange("p g r -> p (g r)"),
+                in_=grouped[("x", m)][:],
+            )
+            codes[("x", m)] = c
+            scales[("x", m)] = s
+
         def quantize(grp, g):
-            if grp == 0:
-                c = const.tile([P, 512], U32, name="xc%d" % g, align_bytes=64)
-                s = const.tile([P, 512], U8, name="xs%d" % g, align_bytes=64)
-            else:
-                c = code_pool.tile([P, 512], U32, name="wc", align_bytes=64)
-                s = code_pool.tile([P, 512], U8, name="ws", align_bytes=64)
+            c = code_pool.tile([P, 512], U32, name="wc", align_bytes=64)
+            s = code_pool.tile([P, 512], U8, name="ws", align_bytes=64)
             nc.vector.quantize_mx(out=c[:].bitcast(E5X4), scales=s[:], in_=grouped[(grp, g)][:])
             codes[(grp, g)] = c
             scales[(grp, g)] = s
@@ -349,11 +412,10 @@ def tile_rlaattention_pa_kernel(tc, x, freqs_cis, Wqkv, out_0, out_1, out_2):
         def mx(n, m, g):
             if g == 0:
                 acc[(n, m)] = acc_pool.tile([P, 512], F32, name="acc")
-            cols = slice(128 * m, 128 * (m + 1))
             nc.tensor.matmul_mx(
                 out=acc[(n, m)][:],
-                lhsT=codes[(0, g)][:, cols].bitcast(E5X4),
-                lhsT_scale=scales[(0, g)][:, cols],
+                lhsT=codes[("x", m)][:, g, :].bitcast(E5X4),
+                lhsT_scale=scales[("x", m)][:, g, :],
                 rhs=codes[(n + 1, g)][:].bitcast(E5X4),
                 rhs_scale=scales[(n + 1, g)][:],
                 start=(g == 0),
@@ -362,7 +424,7 @@ def tile_rlaattention_pa_kernel(tc, x, freqs_cis, Wqkv, out_0, out_1, out_2):
 
         def result_tile(n, m):
             if n >= SINGLE_FROM:
-                res[(n, m)] = work.tile([P, 4, HD], F32, name="res1", bufs=8)
+                res[(n, m)] = work.tile([P, 4, HD], F32, name="res1", bufs=6)
                 return res[(n, m)][:]
             if m % 2 == 0:
                 res[(n, m // 2)] = work.tile([P, 4, 2, HD], F32, name="res")
@@ -407,7 +469,11 @@ def tile_rlaattention_pa_kernel(tc, x, freqs_cis, Wqkv, out_0, out_1, out_2):
 
         for step in PROGRAM:
             kind = step[0]
-            if kind == "T":
+            if kind == "TX":
+                transposes_x(step[1])
+            elif kind == "QX":
+                quantize_x(step[1])
+            elif kind == "T":
                 transposes(step[1], step[2])
             elif kind == "Q":
                 quantize(step[1], step[2])
@@ -421,6 +487,8 @@ def tile_rlaattention_pa_kernel(tc, x, freqs_cis, Wqkv, out_0, out_1, out_2):
                 plain_copy(step[1], step[2])
             elif kind == "L":
                 load_passes(step[1], step[2], step[3])
+            elif kind == "W":
+                keep_warm(step[1])
             elif kind == "O":
                 reorder(step[1], step[2], step[3])
             else:

@@ -15,85 +15,68 @@ P = 128
 HD = 128
 K_PASS = 512
 PASSES = 4
-W_GROUPS = 6
 FLOPS = 2 * 512 * 2048 * 3072
 
-ADD_ON_POOL = True
-SINGLE_FROM = 4
-CODE_BUFS = 12
-REORDERED = ()
-
-LOADS = (
-    ("x", 0, 0, 0),
-    ("k", 1, 0, 1),
-    ("k", 1, 1, 1),
-    ("k", 1, 2, 1),
-    ("k", 1, 3, 1),
-    ("x", 1, 0, 0),
-    ("f", 0, 0, 0),
-    ("x", 2, 0, 0),
-    ("x", 3, 0, 0),
-    ("k", 2, 0, 2),
-    ("k", 2, 2, 2),
-    ("k", 3, 0, 2),
-    ("k", 3, 2, 2),
-    ("k", 4, 0, 2),
-    ("k", 4, 2, 2),
-)
-
 PROGRAM = (
+    ("LX", 0),
+    ("LJ", 1, 0),
+    ("LJ", 1, 1),
+    ("LJ", 1, 2),
+    ("LJ", 1, 3),
+    ("LX", 1),
+    ("LF", 0),
+    ("LX", 2),
+    ("LX", 3),
+    ("L", 2, 0),
+    ("L", 2, 1),
+    ("L", 3, 0),
+    ("L", 3, 1),
+    ("L", 4, 0),
+    ("L", 4, 1),
     ("W", 6),
     ("TX", 0),
     ("W", 1),
     ("QX", 0),
-    ("T", 1, 0),
+    ("TJ", 1, 0),
+    ("W", 1),
+    ("TJ", 1, 1),
+    ("W", 1),
+    ("TJ", 1, 2),
+    ("W", 1),
+    ("TJ", 1, 3),
     ("W", 1),
     ("Q", 1, 0),
-    ("T", 1, 1),
-    ("W", 1),
     ("Q", 1, 1),
-    ("T", 1, 2),
-    ("W", 1),
-    ("Q", 1, 2),
-    ("T", 1, 3),
-    ("W", 1),
-    ("Q", 1, 3),
     ("TX", 1),
+    ("TX", 2),
     ("QX", 1),
-    ("B"),
+    ("B", 0),
+    ("QX", 2),
     ("M", 0, 0, 0),
     ("M", 0, 0, 1),
     ("M", 0, 0, 2),
     ("M", 0, 0, 3),
-    ("TX", 2),
     ("TX", 3),
     ("R", 0, 0),
-    ("A", 0, 0),
-    ("QX", 2),
     ("QX", 3),
     ("M", 0, 1, 0),
     ("M", 0, 1, 1),
     ("M", 0, 1, 2),
     ("M", 0, 1, 3),
     ("T", 2, 0),
-    ("T", 2, 1),
     ("R", 0, 1),
     ("Q", 2, 0),
-    ("A", 0, 1),
-    ("Q", 2, 1),
-    ("L", 5, 0, 2),
+    ("A", 0, 0),
+    ("L", 5, 0),
     ("M", 0, 2, 0),
     ("M", 0, 2, 1),
     ("M", 0, 2, 2),
     ("M", 0, 2, 3),
     ("O", 3, 0, 0),
     ("O", 3, 0, 1),
-    ("T", 2, 2),
-    ("T", 2, 3),
+    ("T", 2, 1),
     ("R", 0, 2),
-    ("Q", 2, 2),
-    ("A", 0, 2),
-    ("Q", 2, 3),
+    ("Q", 2, 1),
     ("M", 0, 3, 0),
     ("M", 0, 3, 1),
     ("M", 0, 3, 2),
@@ -101,31 +84,25 @@ PROGRAM = (
     ("O", 3, 1, 0),
     ("O", 3, 1, 1),
     ("T", 3, 0),
-    ("T", 3, 1),
     ("R", 0, 3),
-    ("Q", 3, 0),
-    ("A", 0, 3),
-    ("Q", 3, 1),
-    ("L", 5, 2, 2),
+    ("A", 0, 1),
+    ("L", 5, 1),
     ("M", 1, 0, 0),
     ("M", 1, 0, 1),
-    ("M", 1, 0, 2),
-    ("M", 1, 0, 3),
     ("M", 1, 1, 0),
     ("M", 1, 1, 1),
+    ("M", 1, 0, 2),
+    ("M", 1, 0, 3),
     ("M", 1, 1, 2),
     ("M", 1, 1, 3),
     ("O", 4, 0, 0),
     ("O", 4, 0, 1),
-    ("T", 3, 2),
-    ("T", 3, 3),
+    ("T", 3, 1),
     ("R", 1, 0),
-    ("Q", 3, 2),
-    ("A", 1, 0),
     ("R", 1, 1),
-    ("Q", 3, 3),
-    ("A", 1, 1),
-    ("L", 6, 0, 2),
+    ("Q", 3, 0),
+    ("A", 1, 0),
+    ("L", 6, 0),
     ("M", 1, 2, 0),
     ("M", 1, 2, 1),
     ("M", 1, 2, 2),
@@ -137,32 +114,26 @@ PROGRAM = (
     ("O", 4, 1, 0),
     ("O", 4, 1, 1),
     ("T", 4, 0),
-    ("T", 4, 1),
     ("R", 1, 2),
-    ("Q", 4, 0),
-    ("A", 1, 2),
     ("R", 1, 3),
-    ("Q", 4, 1),
-    ("A", 1, 3),
-    ("L", 6, 2, 2),
+    ("Q", 3, 1),
+    ("A", 1, 1),
+    ("L", 6, 1),
     ("M", 2, 0, 0),
     ("M", 2, 0, 1),
-    ("M", 2, 0, 2),
-    ("M", 2, 0, 3),
     ("M", 2, 1, 0),
     ("M", 2, 1, 1),
+    ("M", 2, 0, 2),
+    ("M", 2, 0, 3),
     ("M", 2, 1, 2),
     ("M", 2, 1, 3),
     ("O", 5, 0, 0),
     ("O", 5, 0, 1),
-    ("T", 4, 2),
-    ("T", 4, 3),
+    ("T", 4, 1),
     ("R", 2, 0),
-    ("Q", 4, 2),
-    ("A", 2, 0),
     ("R", 2, 1),
-    ("Q", 4, 3),
-    ("A", 2, 1),
+    ("Q", 4, 0),
+    ("A", 2, 0),
     ("M", 2, 2, 0),
     ("M", 2, 2, 1),
     ("M", 2, 2, 2),
@@ -174,31 +145,25 @@ PROGRAM = (
     ("O", 5, 1, 0),
     ("O", 5, 1, 1),
     ("T", 5, 0),
-    ("T", 5, 1),
     ("R", 2, 2),
-    ("Q", 5, 0),
-    ("A", 2, 2),
     ("R", 2, 3),
-    ("Q", 5, 1),
-    ("A", 2, 3),
+    ("Q", 4, 1),
+    ("A", 2, 1),
     ("M", 3, 0, 0),
     ("M", 3, 0, 1),
-    ("M", 3, 0, 2),
-    ("M", 3, 0, 3),
     ("M", 3, 1, 0),
     ("M", 3, 1, 1),
+    ("M", 3, 0, 2),
+    ("M", 3, 0, 3),
     ("M", 3, 1, 2),
     ("M", 3, 1, 3),
     ("O", 6, 0, 0),
     ("O", 6, 0, 1),
-    ("T", 5, 2),
-    ("T", 5, 3),
+    ("T", 5, 1),
     ("R", 3, 0),
-    ("Q", 5, 2),
-    ("A", 3, 0),
     ("R", 3, 1),
-    ("Q", 5, 3),
-    ("A", 3, 1),
+    ("Q", 5, 0),
+    ("A", 3, 0),
     ("M", 3, 2, 0),
     ("M", 3, 2, 1),
     ("M", 3, 2, 2),
@@ -210,50 +175,45 @@ PROGRAM = (
     ("O", 6, 1, 0),
     ("O", 6, 1, 1),
     ("T", 6, 0),
-    ("T", 6, 1),
     ("R", 3, 2),
-    ("Q", 6, 0),
-    ("A", 3, 2),
     ("R", 3, 3),
-    ("Q", 6, 1),
-    ("A", 3, 3),
+    ("Q", 5, 1),
+    ("A", 3, 1),
     ("M", 4, 0, 0),
     ("M", 4, 0, 1),
-    ("M", 4, 0, 2),
-    ("M", 4, 0, 3),
     ("M", 4, 1, 0),
     ("M", 4, 1, 1),
+    ("M", 4, 0, 2),
+    ("M", 4, 0, 3),
     ("M", 4, 1, 2),
     ("M", 4, 1, 3),
-    ("T", 6, 2),
-    ("T", 6, 3),
+    ("T", 6, 1),
     ("R", 4, 0),
-    ("Q", 6, 2),
-    ("A", 4, 0),
     ("R", 4, 1),
-    ("Q", 6, 3),
-    ("A", 4, 1),
+    ("Q", 6, 0),
+    ("Q", 6, 1),
+    ("A", 4, 0, 1),
     ("M", 4, 2, 0),
     ("M", 4, 2, 1),
     ("M", 4, 2, 2),
     ("M", 4, 2, 3),
-    ("R", 4, 2),
-    ("A", 4, 2),
-    ("M", 5, 0, 0),
-    ("M", 5, 0, 1),
-    ("M", 5, 0, 2),
-    ("M", 5, 0, 3),
-    ("C", 5, 0),
     ("M", 4, 3, 0),
     ("M", 4, 3, 1),
     ("M", 4, 3, 2),
     ("M", 4, 3, 3),
+    ("R", 4, 2),
     ("R", 4, 3),
-    ("A", 4, 3),
+    ("A", 4, 1, 1),
+    ("M", 5, 0, 0),
+    ("M", 5, 0, 1),
+    ("M", 5, 0, 2),
+    ("M", 5, 0, 3),
     ("M", 5, 1, 0),
     ("M", 5, 1, 1),
     ("M", 5, 1, 2),
     ("M", 5, 1, 3),
+    ("C", 5, 0, 1),
+    ("C", 5, 1, 1),
     ("M", 5, 2, 0),
     ("M", 5, 2, 1),
     ("M", 5, 2, 2),
@@ -262,9 +222,8 @@ PROGRAM = (
     ("M", 5, 3, 1),
     ("M", 5, 3, 2),
     ("M", 5, 3, 3),
-    ("C", 5, 1),
-    ("C", 5, 2),
-    ("C", 5, 3),
+    ("C", 5, 2, 1),
+    ("C", 5, 3, 1),
 )
 
 
@@ -272,63 +231,62 @@ def tile_rlaattention_pa_kernel(tc, x, freqs_cis, Wqkv, out_0, out_1, out_2):
     nc = tc.nc
     with ExitStack() as ctx:
         const = ctx.enter_context(tc.tile_pool(name="const", bufs=1))
-        raw = ctx.enter_context(tc.tile_pool(name="raw", bufs=1))
-        grp_pool = ctx.enter_context(tc.tile_pool(name="grp", bufs=5))
-        code_pool = ctx.enter_context(tc.tile_pool(name="code", bufs=CODE_BUFS))
-        work = ctx.enter_context(tc.tile_pool(name="work", bufs=3))
+        raw = ctx.enter_context(tc.tile_pool(name="raw", bufs=6))
+        grp_pool = ctx.enter_context(tc.tile_pool(name="grp", bufs=3))
+        code_pool = ctx.enter_context(tc.tile_pool(name="code", bufs=8))
+        work = ctx.enter_context(tc.tile_pool(name="work", bufs=2))
         tp_pool = ctx.enter_context(tc.psum_pool(name="tp", bufs=4))
         acc_pool = ctx.enter_context(tc.psum_pool(name="acc", bufs=4))
         ctx.enter_context(tc.manual_schedule())
 
         x_view = x.flatten_outer_dims().rearrange("(p m) k -> p m k", m=4)
         source = {}
+        grouped = {}
+        codes = {}
+        scales = {}
+        acc = {}
+        prod = {}
+        res = {}
+        idle = {}
+
         f_sb = const.tile([P, 4, HD], BF16, name="f_sb")
-
-        def rows_of(grp):
-            if grp == 0:
-                return x_view
-            return Wqkv[(grp - 1) * 512 : grp * 512, :].rearrange("(j p) k -> p j k", p=P)
-
-        def load_passes(grp, g0, count):
-            t = raw.tile([P, 4, K_PASS * count], BF16, name="rawk%d_%d" % (grp, g0))
-            nc.sync.dma_start(out=t[:], in_=rows_of(grp)[:, :, K_PASS * g0 : K_PASS * (g0 + count)])
-            for g in range(g0, g0 + count):
-                for j in range(4):
-                    source[(grp, g, j)] = (t, j, 256 * (g - g0), 2)
-
-        def load_x(m):
-            t = raw.tile([P, K_PASS * PASSES], BF16, name="rawx%d" % m)
-            nc.sync.dma_start(out=t[:], in_=x_view[:, m, :])
-            source[("x", m)] = t
-
-        def load(entry):
-            if entry[0] == "x":
-                load_x(entry[1])
-            elif entry[0] == "f":
-                nc.sync.dma_start(out=f_sb[:], in_=freqs_cis.rearrange("(p m) d -> p m d", m=4))
-            else:
-                load_passes(entry[1], entry[2], entry[3])
-
-        for entry in LOADS:
-            load(entry)
-
         ident = const.tile([P, P], F32, name="ident")
         make_identity(nc, ident[:])
         warm = const.tile([P, 1], F32, name="warm")
         nc.scalar.copy(out=warm[:], in_=ident[:, 0:1])
-
         zeros = const.tile([P, 512], BF16, name="zeros")
         nc.vector.memset(zeros[:], 0.0)
-        idle = {}
+        tab_a = const.tile([P, 4, HD], F32, name="tab_a")
+        tab_b = const.tile([P, 4, HD], F32, name="tab_b")
+
+        def w_rows(grp):
+            return Wqkv[(grp - 1) * 512 : grp * 512, :].rearrange("(j p) k -> p j k", p=P)
+
+        def load_f():
+            nc.sync.dma_start(out=f_sb[:], in_=freqs_cis.rearrange("(p m) d -> p m d", m=4))
+
+        def load_x(m):
+            t = const.tile([P, K_PASS * PASSES], BF16, name="rawx%d" % m)
+            nc.sync.dma_start(out=t[:], in_=x_view[:, m, :])
+            source[("x", m)] = t
+
+        def load_row_tile(grp, j):
+            t = const.tile([P, K_PASS * PASSES], BF16, name="rawj%d" % j)
+            nc.sync.dma_start(out=t[:], in_=w_rows(grp)[:, j, :])
+            for gp in range(2):
+                source[(grp, gp, j)] = (t[:].bitcast(F32)[:, 512 * gp : 512 * (gp + 1)], 2)
+
+        def load_half(grp, gp):
+            t = raw.tile([P, 4, 2 * K_PASS], BF16, name="rawk")
+            nc.sync.dma_start(out=t[:], in_=w_rows(grp)[:, :, 2 * K_PASS * gp : 2 * K_PASS * (gp + 1)])
+            for j in range(4):
+                source[(grp, gp, j)] = (t[:, j, :].bitcast(F32), 2)
 
         def keep_warm(count):
             if len(idle) == 0:
                 idle[0] = acc_pool.tile([P, 512], F32, name="acc")
             for i in range(count):
                 nc.tensor.matmul(out=idle[0][:], lhsT=zeros[:, 0:P], rhs=zeros[:], start=True, stop=True)
-
-        tab_a = const.tile([P, 4, HD], F32, name="tab_a")
-        tab_b = const.tile([P, 4, HD], F32, name="tab_b")
 
         def build_tables():
             f_pairs = f_sb[:].rearrange("p m (j e) -> p m j e", e=2)
@@ -339,57 +297,65 @@ def tile_rlaattention_pa_kernel(tc, x, freqs_cis, Wqkv, out_0, out_1, out_2):
             nc.vector.tensor_copy(out=b_pairs[:, :, :, 0], in_=f_pairs[:, :, :, 0])
             nc.vector.tensor_scalar_mul(out=b_pairs[:, :, :, 1], in0=f_pairs[:, :, :, 0], scalar1=-1.0)
 
-        grouped = {}
-        codes = {}
-        scales = {}
-        acc = {}
-        prod = {}
-        res = {}
-
         def reorder(grp, gp, j):
-            t, jj, w0, step = source[(grp, 2 * gp, j)]
-            ro = work.tile([P, 2, 2, 128], F32, name="ro", bufs=6)
-            words = t[:, jj, :].bitcast(F32)[:, w0 : w0 + 512]
+            words, step = source[(grp, gp, j)]
+            ro = work.tile([P, 2, 2, 128], F32, name="ro", bufs=4)
             nc.scalar.copy(out=ro[:], in_=words.rearrange("r (g p u) -> r g u p", g=2, u=2))
-            for gg in range(2):
-                source[(grp, 2 * gp + gg, j)] = (ro, gg, 0, 1)
+            source[(grp, gp, j)] = (ro[:].rearrange("r g u p -> r (g u p)"), 1)
 
-        def transposes(grp, g):
-            gt = grp_pool.tile([P, 4 * 512], BF16, name="gt", align_bytes=64)
-            gw = gt[:].bitcast(F32).rearrange("p (r u) -> p r u", u=2)
-            for rp in range(2):
-                bank = tp_pool.tile([P, 512], F32, name="bank")
-                for u in range(2):
-                    for jj in range(2):
-                        t, j, w0, step = source[(grp, g, 2 * rp + jj)]
-                        c0 = 256 * u + 128 * jj
-                        if step == 2:
-                            words = t[:, j, :].bitcast(F32)[:, w0 + u : w0 + 256 : 2]
-                        else:
-                            words = t[:, j, u, :]
-                        nc.tensor.transpose(bank[:, c0 : c0 + 128], words, ident[:])
-                nc.scalar.copy(
-                    out=gw[:, 256 * rp : 256 * (rp + 1), :],
-                    in_=bank[:].rearrange("p (u r) -> p r u", u=2),
-                )
-            grouped[(grp, g)] = gt
+        def word_columns(entry, gg, u):
+            words, step = entry
+            if step == 2:
+                return words[:, 256 * gg + u : 256 * (gg + 1) : 2]
+            return words[:, 256 * gg + 128 * u : 256 * gg + 128 * (u + 1)]
+
+        def pair_tile(grp, gp):
+            if (grp, gp) not in grouped:
+                grouped[(grp, gp)] = grp_pool.tile([P, 2 * 4 * 512], BF16, name="gt", align_bytes=64)
+            return grouped[(grp, gp)][:].bitcast(F32).rearrange("p (g r u) -> p g r u", g=2, u=2)
 
         def transposes_x(m):
-            words = source[("x", m)][:].bitcast(F32)
-            gt = grp_pool.tile([P, 4 * 512], BF16, name="gt", align_bytes=64)
+            words = (source[("x", m)][:].bitcast(F32), 2)
+            gt = grp_pool.tile([P, 4 * 512], BF16, name="gx", align_bytes=64, bufs=2)
             gw = gt[:].bitcast(F32).rearrange("p (g r u) -> p g r u", g=PASSES, u=2)
             for gp in range(2):
                 bank = tp_pool.tile([P, 512], F32, name="bank")
                 for gg in range(2):
                     for u in range(2):
-                        g = 2 * gp + gg
                         c0 = 256 * gg + 128 * u
-                        nc.tensor.transpose(bank[:, c0 : c0 + 128], words[:, 256 * g + u : 256 * (g + 1) : 2], ident[:])
+                        nc.tensor.transpose(bank[:, c0 : c0 + 128], word_columns(words, 2 * gp + gg, u), ident[:])
                 nc.scalar.copy(
                     out=gw[:, 2 * gp : 2 * gp + 2, :, :],
                     in_=bank[:].rearrange("p (g u r) -> p g r u", g=2, u=2),
                 )
             grouped[("x", m)] = gt
+
+        def transposes_row_tile(grp, j):
+            for gp in range(2):
+                bank = tp_pool.tile([P, 512], F32, name="bank")
+                for gg in range(2):
+                    for u in range(2):
+                        c0 = 256 * gg + 128 * u
+                        nc.tensor.transpose(bank[:, c0 : c0 + 128], word_columns(source[(grp, gp, j)], gg, u), ident[:])
+                nc.scalar.copy(
+                    out=pair_tile(grp, gp)[:, :, 128 * j : 128 * (j + 1), :],
+                    in_=bank[:].rearrange("p (g u r) -> p g r u", g=2, u=2),
+                )
+
+        def transposes(grp, gp):
+            for gg in range(2):
+                for rp in range(2):
+                    bank = tp_pool.tile([P, 512], F32, name="bank")
+                    for u in range(2):
+                        for jj in range(2):
+                            c0 = 256 * u + 128 * jj
+                            nc.tensor.transpose(
+                                bank[:, c0 : c0 + 128], word_columns(source[(grp, gp, 2 * rp + jj)], gg, u), ident[:]
+                            )
+                    nc.scalar.copy(
+                        out=pair_tile(grp, gp)[:, gg, 256 * rp : 256 * (rp + 1), :],
+                        in_=bank[:].rearrange("p (u r) -> p r u", u=2),
+                    )
 
         def quantize_x(m):
             c = const.tile([P, PASSES, P], U32, name="xc%d" % m, align_bytes=64)
@@ -402,12 +368,16 @@ def tile_rlaattention_pa_kernel(tc, x, freqs_cis, Wqkv, out_0, out_1, out_2):
             codes[("x", m)] = c
             scales[("x", m)] = s
 
-        def quantize(grp, g):
-            c = code_pool.tile([P, 512], U32, name="wc", align_bytes=64)
-            s = code_pool.tile([P, 512], U8, name="ws", align_bytes=64)
-            nc.vector.quantize_mx(out=c[:].bitcast(E5X4), scales=s[:], in_=grouped[(grp, g)][:])
-            codes[(grp, g)] = c
-            scales[(grp, g)] = s
+        def quantize(grp, gp):
+            c = code_pool.tile([P, 2, 512], U32, name="wc", align_bytes=64)
+            s = code_pool.tile([P, 2, 512], U8, name="ws", align_bytes=64)
+            nc.vector.quantize_mx(
+                out=c[:].rearrange("p g r -> p (g r)").bitcast(E5X4),
+                scales=s[:].rearrange("p g r -> p (g r)"),
+                in_=grouped[(grp, gp)][:],
+            )
+            codes[(grp, gp)] = c
+            scales[(grp, gp)] = s
 
         def mx(n, m, g):
             if g == 0:
@@ -416,65 +386,106 @@ def tile_rlaattention_pa_kernel(tc, x, freqs_cis, Wqkv, out_0, out_1, out_2):
                 out=acc[(n, m)][:],
                 lhsT=codes[("x", m)][:, g, :].bitcast(E5X4),
                 lhsT_scale=scales[("x", m)][:, g, :],
-                rhs=codes[(n + 1, g)][:].bitcast(E5X4),
-                rhs_scale=scales[(n + 1, g)][:],
+                rhs=codes[(n + 1, g // 2)][:, g % 2, :].bitcast(E5X4),
+                rhs_scale=scales[(n + 1, g // 2)][:, g % 2, :],
                 start=(g == 0),
                 stop=(g == PASSES - 1),
             )
 
-        def result_tile(n, m):
-            if n >= SINGLE_FROM:
-                res[(n, m)] = work.tile([P, 4, HD], F32, name="res1", bufs=6)
-                return res[(n, m)][:]
-            if m % 2 == 0:
-                res[(n, m // 2)] = work.tile([P, 4, 2, HD], F32, name="res")
-            return res[(n, m // 2)][:, :, m % 2, :]
-
         def rope_products(n, m):
+            if m % 2 == 0:
+                m1 = work.tile([P, 4, 2, HD], F32, name="m1")
+                m2 = work.tile([P, 4, 2, HD], F32, name="m2")
+                prod[(n, m // 2)] = (m1, m2)
+            m1, m2 = prod[(n, m // 2)]
             a3 = acc[(n, m)][:].rearrange("p (h c) -> p h c", h=4)
-            m1 = work.tile([P, 4, HD], F32, name="m1")
-            m2 = work.tile([P, 4, HD], F32, name="m2")
-            nc.vector.tensor_tensor(out=m1[:], in0=a3, in1=tab_a[:, m : m + 1, :].to_broadcast([P, 4, HD]), op=MULT)
-            nc.vector.tensor_tensor(out=m2[:], in0=a3, in1=tab_b[:, m : m + 1, :].to_broadcast([P, 4, HD]), op=MULT)
-            prod[(n, m)] = (m1, m2)
+            nc.vector.tensor_tensor(
+                out=m1[:, :, m % 2, :], in0=a3, in1=tab_a[:, m : m + 1, :].to_broadcast([P, 4, HD]), op=MULT
+            )
+            nc.vector.tensor_tensor(
+                out=m2[:, :, m % 2, :], in0=a3, in1=tab_b[:, m : m + 1, :].to_broadcast([P, 4, HD]), op=MULT
+            )
 
-        def rope_add(n, m):
-            m1, m2 = prod[(n, m)]
-            eng = nc.gpsimd if ADD_ON_POOL else nc.vector
+        def out_rows(n):
+            if n < 4:
+                return out_0[0, 4 * n : 4 * n + 4]
+            if n == 4:
+                return out_1[0]
+            return out_2[0]
+
+        def store_pair(queue, n, mp):
+            view = out_rows(n).rearrange("h (p a b) d -> p a h (b d)", a=2, b=2)
+            queue.dma_start(out=view[:, mp], in_=res[(n, mp)][:].rearrange("p h b d -> p h (b d)"))
+
+        def rope_add(n, mp, on_vector):
+            m1, m2 = prod[(n, mp)]
+            eng = nc.vector if on_vector else nc.gpsimd
+            res[(n, mp)] = work.tile([P, 4, 2, HD], F32, name="res", bufs=3)
             eng.tensor_tensor(
-                out=result_tile(n, m).rearrange("p h (j e) -> p h j e", e=2),
-                in0=m1[:].rearrange("p h (j e) -> p h j e", e=2),
-                in1=m2[:].rearrange("p h (j e) -> p h j e", e=2)[:, :, :, ::-1],
+                out=res[(n, mp)][:].rearrange("p h b (j e) -> p (h b j) e", e=2),
+                in0=m1[:].rearrange("p h b (j e) -> p (h b j) e", e=2),
+                in1=m2[:].rearrange("p h b (j e) -> p (h b j) e", e=2)[:, :, ::-1],
                 op=ADD,
             )
-            store(nc.sync, n, m)
+            store_pair(nc.sync, n, mp)
 
-        def plain_copy(n, m):
-            nc.scalar.copy(out=result_tile(n, m), in_=acc[(n, m)][:].rearrange("p (h c) -> p h c", h=4))
-            store(nc.scalar, n, m)
+        def rope_products_one(n, m):
+            m1 = work.tile([P, 4, HD], F32, name="m1s", bufs=3)
+            m2 = work.tile([P, 4, HD], F32, name="m2s", bufs=3)
+            prod[(n, m, 1)] = (m1, m2)
+            a3 = acc[(n, m)][:].rearrange("p (h c) -> p h c", h=4)
+            nc.vector.tensor_tensor(out=m1[:], in0=a3, in1=tab_a[:, m : m + 1, :].to_broadcast([P, 4, HD]), op=MULT)
+            nc.vector.tensor_tensor(out=m2[:], in0=a3, in1=tab_b[:, m : m + 1, :].to_broadcast([P, 4, HD]), op=MULT)
 
-        def store(queue, n, m):
-            if n < 4:
-                dst = out_0[0, 4 * n : 4 * n + 4]
-            elif n == 4:
-                dst = out_1[0]
+        def rope_add_one(n, m, on_vector):
+            m1, m2 = prod[(n, m, 1)]
+            t = work.tile([P, 4, HD], F32, name="res1", bufs=4)
+            eng = nc.vector if on_vector else nc.gpsimd
+            eng.tensor_tensor(
+                out=t[:].rearrange("p h (j e) -> p (h j) e", e=2),
+                in0=m1[:].rearrange("p h (j e) -> p (h j) e", e=2),
+                in1=m2[:].rearrange("p h (j e) -> p (h j) e", e=2)[:, :, ::-1],
+                op=ADD,
+            )
+            nc.sync.dma_start(out=out_rows(n).rearrange("h (p m) d -> p m h d", m=4)[:, m], in_=t[:])
+
+        def plain_copy(n, m, alone):
+            a3 = acc[(n, m)][:].rearrange("p (h c) -> p h c", h=4)
+            if alone:
+                t = work.tile([P, 4, HD], F32, name="res1", bufs=4)
+                nc.scalar.copy(out=t[:], in_=a3)
+                nc.scalar.dma_start(out=out_rows(n).rearrange("h (p m) d -> p m h d", m=4)[:, m], in_=t[:])
             else:
-                dst = out_2[0]
-            if n >= SINGLE_FROM:
-                view = dst.rearrange("h (p m) d -> p m h d", m=4)
-                queue.dma_start(out=view[:, m], in_=res[(n, m)][:])
-            elif m % 2 == 1:
-                view = dst.rearrange("h (p a b) d -> p a h (b d)", a=2, b=2)
-                queue.dma_start(out=view[:, m // 2], in_=res[(n, m // 2)][:].rearrange("p h b d -> p h (b d)"))
+                if m % 2 == 0:
+                    res[(n, m // 2)] = work.tile([P, 4, 2, HD], F32, name="res", bufs=3)
+                nc.scalar.copy(out=res[(n, m // 2)][:, :, m % 2, :], in_=a3)
+                if m % 2 == 1:
+                    store_pair(nc.scalar, n, m // 2)
 
         for step in PROGRAM:
             kind = step[0]
-            if kind == "TX":
+            if kind == "LX":
+                load_x(step[1])
+            elif kind == "LF":
+                load_f()
+            elif kind == "LJ":
+                load_row_tile(step[1], step[2])
+            elif kind == "L":
+                load_half(step[1], step[2])
+            elif kind == "W":
+                keep_warm(step[1])
+            elif kind == "B":
+                build_tables()
+            elif kind == "O":
+                reorder(step[1], step[2], step[3])
+            elif kind == "TX":
                 transposes_x(step[1])
-            elif kind == "QX":
-                quantize_x(step[1])
+            elif kind == "TJ":
+                transposes_row_tile(step[1], step[2])
             elif kind == "T":
                 transposes(step[1], step[2])
+            elif kind == "QX":
+                quantize_x(step[1])
             elif kind == "Q":
                 quantize(step[1], step[2])
             elif kind == "M":
@@ -482,14 +493,10 @@ def tile_rlaattention_pa_kernel(tc, x, freqs_cis, Wqkv, out_0, out_1, out_2):
             elif kind == "R":
                 rope_products(step[1], step[2])
             elif kind == "A":
-                rope_add(step[1], step[2])
+                rope_add(step[1], step[2], len(step) > 3)
+            elif kind == "R1":
+                rope_products_one(step[1], step[2])
+            elif kind == "A1":
+                rope_add_one(step[1], step[2], step[3] == 1)
             elif kind == "C":
-                plain_copy(step[1], step[2])
-            elif kind == "L":
-                load_passes(step[1], step[2], step[3])
-            elif kind == "W":
-                keep_warm(step[1])
-            elif kind == "O":
-                reorder(step[1], step[2], step[3])
-            else:
-                build_tables()
+                plain_copy(step[1], step[2], step[3] == 1)

@@ -256,8 +256,7 @@ def tile_rlaattention_pa_kernel(tc, x, freqs_cis, Wqkv, out_0, out_1, out_2):
         nc.scalar.copy(out=warm[:], in_=ident[:, 0:1])
         zeros = const.tile([P, 512], BF16, name="zeros")
         nc.vector.memset(zeros[:], 0.0)
-        tab_a = const.tile([P, 4, HD], F32, name="tab_a")
-        tab_b = const.tile([P, 4, HD], F32, name="tab_b")
+        tab = const.tile([P, 2, 4, HD], F32, name="tab")
 
         def w_rows(grp):
             return Wqkv[(grp - 1) * 512 : grp * 512, :].rearrange("(j p) k -> p j k", p=P)
@@ -290,8 +289,8 @@ def tile_rlaattention_pa_kernel(tc, x, freqs_cis, Wqkv, out_0, out_1, out_2):
 
         def build_tables():
             f_pairs = f_sb[:].rearrange("p m (j e) -> p m j e", e=2)
-            a_pairs = tab_a[:].rearrange("p m (j e) -> p m j e", e=2)
-            b_pairs = tab_b[:].rearrange("p m (j e) -> p m j e", e=2)
+            a_pairs = tab[:, 0].rearrange("p m (j e) -> p m j e", e=2)
+            b_pairs = tab[:, 1].rearrange("p m (j e) -> p m j e", e=2)
             nc.vector.tensor_copy(out=a_pairs[:, :, :, 0], in_=f_pairs[:, :, :, 1])
             nc.vector.tensor_copy(out=a_pairs[:, :, :, 1], in_=f_pairs[:, :, :, 1])
             nc.vector.tensor_copy(out=b_pairs[:, :, :, 0], in_=f_pairs[:, :, :, 0])
@@ -394,16 +393,13 @@ def tile_rlaattention_pa_kernel(tc, x, freqs_cis, Wqkv, out_0, out_1, out_2):
 
         def rope_products(n, m):
             if m % 2 == 0:
-                m1 = work.tile([P, 4, 2, HD], F32, name="m1")
-                m2 = work.tile([P, 4, 2, HD], F32, name="m2")
-                prod[(n, m // 2)] = (m1, m2)
-            m1, m2 = prod[(n, m // 2)]
-            a3 = acc[(n, m)][:].rearrange("p (h c) -> p h c", h=4)
+                prod[(n, m // 2)] = work.tile([P, 2, 4, 2, HD], F32, name="m12")
+            m12 = prod[(n, m // 2)]
             nc.vector.tensor_tensor(
-                out=m1[:, :, m % 2, :], in0=a3, in1=tab_a[:, m : m + 1, :].to_broadcast([P, 4, HD]), op=MULT
-            )
-            nc.vector.tensor_tensor(
-                out=m2[:, :, m % 2, :], in0=a3, in1=tab_b[:, m : m + 1, :].to_broadcast([P, 4, HD]), op=MULT
+                out=m12[:, :, :, m % 2, :],
+                in0=acc[(n, m)][:].rearrange("p (o h c) -> p o h c", o=1, h=4).to_broadcast([P, 2, 4, HD]),
+                in1=tab[:, :, m : m + 1, :].to_broadcast([P, 2, 4, HD]),
+                op=MULT,
             )
 
         def out_rows(n):
@@ -418,36 +414,16 @@ def tile_rlaattention_pa_kernel(tc, x, freqs_cis, Wqkv, out_0, out_1, out_2):
             queue.dma_start(out=view[:, mp], in_=res[(n, mp)][:].rearrange("p h b d -> p h (b d)"))
 
         def rope_add(n, mp, on_vector):
-            m1, m2 = prod[(n, mp)]
+            m12 = prod[(n, mp)]
             eng = nc.vector if on_vector else nc.gpsimd
             res[(n, mp)] = work.tile([P, 4, 2, HD], F32, name="res", bufs=3)
             eng.tensor_tensor(
                 out=res[(n, mp)][:].rearrange("p h b (j e) -> p (h b j) e", e=2),
-                in0=m1[:].rearrange("p h b (j e) -> p (h b j) e", e=2),
-                in1=m2[:].rearrange("p h b (j e) -> p (h b j) e", e=2)[:, :, ::-1],
+                in0=m12[:, 0].rearrange("p h b (j e) -> p (h b j) e", e=2),
+                in1=m12[:, 1].rearrange("p h b (j e) -> p (h b j) e", e=2)[:, :, ::-1],
                 op=ADD,
             )
             store_pair(nc.sync, n, mp)
-
-        def rope_products_one(n, m):
-            m1 = work.tile([P, 4, HD], F32, name="m1s", bufs=3)
-            m2 = work.tile([P, 4, HD], F32, name="m2s", bufs=3)
-            prod[(n, m, 1)] = (m1, m2)
-            a3 = acc[(n, m)][:].rearrange("p (h c) -> p h c", h=4)
-            nc.vector.tensor_tensor(out=m1[:], in0=a3, in1=tab_a[:, m : m + 1, :].to_broadcast([P, 4, HD]), op=MULT)
-            nc.vector.tensor_tensor(out=m2[:], in0=a3, in1=tab_b[:, m : m + 1, :].to_broadcast([P, 4, HD]), op=MULT)
-
-        def rope_add_one(n, m, on_vector):
-            m1, m2 = prod[(n, m, 1)]
-            t = work.tile([P, 4, HD], F32, name="res1", bufs=4)
-            eng = nc.vector if on_vector else nc.gpsimd
-            eng.tensor_tensor(
-                out=t[:].rearrange("p h (j e) -> p (h j) e", e=2),
-                in0=m1[:].rearrange("p h (j e) -> p (h j) e", e=2),
-                in1=m2[:].rearrange("p h (j e) -> p (h j) e", e=2)[:, :, ::-1],
-                op=ADD,
-            )
-            nc.sync.dma_start(out=out_rows(n).rearrange("h (p m) d -> p m h d", m=4)[:, m], in_=t[:])
 
         def plain_copy(n, m, alone):
             a3 = acc[(n, m)][:].rearrange("p (h c) -> p h c", h=4)
@@ -494,9 +470,5 @@ def tile_rlaattention_pa_kernel(tc, x, freqs_cis, Wqkv, out_0, out_1, out_2):
                 rope_products(step[1], step[2])
             elif kind == "A":
                 rope_add(step[1], step[2], len(step) > 3)
-            elif kind == "R1":
-                rope_products_one(step[1], step[2])
-            elif kind == "A1":
-                rope_add_one(step[1], step[2], step[3] == 1)
             elif kind == "C":
                 plain_copy(step[1], step[2], step[3] == 1)

@@ -95,8 +95,7 @@ PROGRAM = (
     ("M", 1, 0, 3),
     ("M", 1, 1, 2),
     ("M", 1, 1, 3),
-    ("O", 4, 0, 0),
-    ("O", 4, 0, 1),
+    ("OS", 4, 0, 6),
     ("T", 3, 1),
     ("R", 1, 0),
     ("R", 1, 1),
@@ -111,8 +110,7 @@ PROGRAM = (
     ("M", 1, 3, 1),
     ("M", 1, 3, 2),
     ("M", 1, 3, 3),
-    ("O", 4, 1, 0),
-    ("O", 4, 1, 1),
+    ("OS", 4, 1, 6),
     ("T", 4, 0),
     ("R", 1, 2),
     ("R", 1, 3),
@@ -127,8 +125,7 @@ PROGRAM = (
     ("M", 2, 0, 3),
     ("M", 2, 1, 2),
     ("M", 2, 1, 3),
-    ("O", 5, 0, 0),
-    ("O", 5, 0, 1),
+    ("OS", 5, 0, 6),
     ("T", 4, 1),
     ("R", 2, 0),
     ("R", 2, 1),
@@ -142,8 +139,7 @@ PROGRAM = (
     ("M", 2, 3, 1),
     ("M", 2, 3, 2),
     ("M", 2, 3, 3),
-    ("O", 5, 1, 0),
-    ("O", 5, 1, 1),
+    ("OS", 5, 1, 6),
     ("T", 5, 0),
     ("R", 2, 2),
     ("R", 2, 3),
@@ -157,8 +153,7 @@ PROGRAM = (
     ("M", 3, 0, 3),
     ("M", 3, 1, 2),
     ("M", 3, 1, 3),
-    ("O", 6, 0, 0),
-    ("O", 6, 0, 1),
+    ("OS", 6, 0, 6),
     ("T", 5, 1),
     ("R", 3, 0),
     ("R", 3, 1),
@@ -172,8 +167,7 @@ PROGRAM = (
     ("M", 3, 3, 1),
     ("M", 3, 3, 2),
     ("M", 3, 3, 3),
-    ("O", 6, 1, 0),
-    ("O", 6, 1, 1),
+    ("OS", 6, 1, 6),
     ("T", 6, 0),
     ("R", 3, 2),
     ("R", 3, 3),
@@ -248,6 +242,8 @@ def tile_rlaattention_pa_kernel(tc, x, freqs_cis, Wqkv, out_0, out_1, out_2):
         prod = {}
         res = {}
         idle = {}
+        halves = {}
+        in_order = {}
 
         f_sb = const.tile([P, 4, HD], BF16, name="f_sb")
         ident = const.tile([P, P], F32, name="ident")
@@ -278,6 +274,7 @@ def tile_rlaattention_pa_kernel(tc, x, freqs_cis, Wqkv, out_0, out_1, out_2):
         def load_half(grp, gp):
             t = raw.tile([P, 4, 2 * K_PASS], BF16, name="rawk")
             nc.sync.dma_start(out=t[:], in_=w_rows(grp)[:, :, 2 * K_PASS * gp : 2 * K_PASS * (gp + 1)])
+            halves[(grp, gp)] = t
             for j in range(4):
                 source[(grp, gp, j)] = (t[:, j, :].bitcast(F32), 2)
 
@@ -301,6 +298,13 @@ def tile_rlaattention_pa_kernel(tc, x, freqs_cis, Wqkv, out_0, out_1, out_2):
             ro = work.tile([P, 2, 2, 128], F32, name="ro", bufs=4)
             nc.scalar.copy(out=ro[:], in_=words.rearrange("r (g p u) -> r g u p", g=2, u=2))
             source[(grp, gp, j)] = (ro[:].rearrange("r g u p -> r (g u p)"), 1)
+
+        def reorder_units(grp, gp, count):
+            words = halves[(grp, gp)][:].bitcast(F32).rearrange("r j w -> r (j w)")[:, 0 : 256 * count]
+            ro = work.tile([P, count, 2, 128], F32, name="rs", bufs=2)
+            nc.scalar.copy(out=ro[:], in_=words.rearrange("r (c p u) -> r c u p", c=count, u=2))
+            for unit in range(count):
+                in_order[(grp, gp, unit)] = ro
 
         def word_columns(entry, gg, u):
             words, step = entry
@@ -348,9 +352,12 @@ def tile_rlaattention_pa_kernel(tc, x, freqs_cis, Wqkv, out_0, out_1, out_2):
                     for u in range(2):
                         for jj in range(2):
                             c0 = 256 * u + 128 * jj
-                            nc.tensor.transpose(
-                                bank[:, c0 : c0 + 128], word_columns(source[(grp, gp, 2 * rp + jj)], gg, u), ident[:]
-                            )
+                            unit = 2 * (2 * rp + jj) + gg
+                            if (grp, gp, unit) in in_order:
+                                columns = in_order[(grp, gp, unit)][:, unit, u, :]
+                            else:
+                                columns = word_columns(source[(grp, gp, 2 * rp + jj)], gg, u)
+                            nc.tensor.transpose(bank[:, c0 : c0 + 128], columns, ident[:])
                     nc.scalar.copy(
                         out=pair_tile(grp, gp)[:, gg, 256 * rp : 256 * (rp + 1), :],
                         in_=bank[:].rearrange("p (u r) -> p r u", u=2),
@@ -454,6 +461,8 @@ def tile_rlaattention_pa_kernel(tc, x, freqs_cis, Wqkv, out_0, out_1, out_2):
                 build_tables()
             elif kind == "O":
                 reorder(step[1], step[2], step[3])
+            elif kind == "OS":
+                reorder_units(step[1], step[2], step[3])
             elif kind == "TX":
                 transposes_x(step[1])
             elif kind == "TJ":

@@ -290,8 +290,8 @@ def tile_rlaattention_pa_kernel(tc, x, freqs_cis, Wqkv, out_0, out_1, out_2):
             b_pairs = tab[:, 1].rearrange("p m (j e) -> p m j e", e=2)
             nc.vector.tensor_copy(out=a_pairs[:, :, :, 0], in_=f_pairs[:, :, :, 1])
             nc.vector.tensor_copy(out=a_pairs[:, :, :, 1], in_=f_pairs[:, :, :, 1])
-            nc.vector.tensor_copy(out=b_pairs[:, :, :, 0], in_=f_pairs[:, :, :, 0])
-            nc.vector.tensor_scalar_mul(out=b_pairs[:, :, :, 1], in0=f_pairs[:, :, :, 0], scalar1=-1.0)
+            nc.vector.tensor_copy(out=b_pairs[:, :, :, 1], in_=f_pairs[:, :, :, 0])
+            nc.vector.tensor_scalar_mul(out=b_pairs[:, :, :, 0], in0=f_pairs[:, :, :, 0], scalar1=-1.0)
 
         def reorder(grp, gp, j):
             words, step = source[(grp, gp, j)]
@@ -403,9 +403,15 @@ def tile_rlaattention_pa_kernel(tc, x, freqs_cis, Wqkv, out_0, out_1, out_2):
                 prod[(n, m // 2)] = work.tile([P, 2, 4, 2, HD], F32, name="m12")
             m12 = prod[(n, m // 2)]
             nc.vector.tensor_tensor(
-                out=m12[:, :, :, m % 2, :],
-                in0=acc[(n, m)][:].rearrange("p (o h c) -> p o h c", o=1, h=4).to_broadcast([P, 2, 4, HD]),
-                in1=tab[:, :, m : m + 1, :].to_broadcast([P, 2, 4, HD]),
+                out=m12[:, 0, :, m % 2, :],
+                in0=acc[(n, m)][:].rearrange("p (h c) -> p h c", h=4),
+                in1=tab[:, 0, m : m + 1, :].to_broadcast([P, 4, HD]),
+                op=MULT,
+            )
+            nc.vector.tensor_tensor(
+                out=m12[:, 1, :, m % 2, :].rearrange("p h (j e) -> p h j e", e=2),
+                in0=acc[(n, m)][:].rearrange("p (h j e) -> p h j e", h=4, e=2)[:, :, :, ::-1],
+                in1=tab[:, 1, m : m + 1, :].rearrange("p o (j e) -> p o j e", e=2).to_broadcast([P, 4, HD // 2, 2]),
                 op=MULT,
             )
 
@@ -425,9 +431,9 @@ def tile_rlaattention_pa_kernel(tc, x, freqs_cis, Wqkv, out_0, out_1, out_2):
             eng = nc.vector if on_vector else nc.gpsimd
             res[(n, mp)] = work.tile([P, 4, 2, HD], F32, name="res", bufs=3)
             eng.tensor_tensor(
-                out=res[(n, mp)][:].rearrange("p h b (j e) -> p (h b j) e", e=2),
-                in0=m12[:, 0].rearrange("p h b (j e) -> p (h b j) e", e=2),
-                in1=m12[:, 1].rearrange("p h b (j e) -> p (h b j) e", e=2)[:, :, ::-1],
+                out=res[(n, mp)][:].rearrange("p h b d -> p (h b d)"),
+                in0=m12[:, 0].rearrange("p h b d -> p (h b d)"),
+                in1=m12[:, 1].rearrange("p h b d -> p (h b d)"),
                 op=ADD,
             )
             store_pair(nc.sync, n, mp)

@@ -72,8 +72,6 @@ PROGRAM = (
     ("M", 0, 2, 1),
     ("M", 0, 2, 2),
     ("M", 0, 2, 3),
-    ("O", 3, 0, 0),
-    ("O", 3, 0, 1),
     ("T", 2, 1),
     ("R", 0, 2),
     ("Q", 2, 1),
@@ -81,9 +79,9 @@ PROGRAM = (
     ("M", 0, 3, 1),
     ("M", 0, 3, 2),
     ("M", 0, 3, 3),
-    ("O", 3, 1, 0),
-    ("O", 3, 1, 1),
-    ("T", 3, 0),
+    ("O", 3, 0, 0),
+    ("O", 3, 0, 1),
+    ("T", 3, 0, 1),
     ("R", 0, 3),
     ("A", 0, 1),
     ("L", 5, 1),
@@ -95,7 +93,8 @@ PROGRAM = (
     ("M", 1, 0, 3),
     ("M", 1, 1, 2),
     ("M", 1, 1, 3),
-    ("OS", 4, 0, 6),
+    ("O", 3, 1, 0),
+    ("O", 3, 1, 1),
     ("T", 3, 1),
     ("R", 1, 0),
     ("R", 1, 1),
@@ -110,7 +109,8 @@ PROGRAM = (
     ("M", 1, 3, 1),
     ("M", 1, 3, 2),
     ("M", 1, 3, 3),
-    ("OS", 4, 1, 6),
+    ("OS", 4, 0, 0),
+    ("OS", 4, 0, 1),
     ("T", 4, 0),
     ("R", 1, 2),
     ("R", 1, 3),
@@ -125,7 +125,8 @@ PROGRAM = (
     ("M", 2, 0, 3),
     ("M", 2, 1, 2),
     ("M", 2, 1, 3),
-    ("OS", 5, 0, 6),
+    ("OS", 4, 1, 0),
+    ("OS", 4, 1, 1),
     ("T", 4, 1),
     ("R", 2, 0),
     ("R", 2, 1),
@@ -139,7 +140,8 @@ PROGRAM = (
     ("M", 2, 3, 1),
     ("M", 2, 3, 2),
     ("M", 2, 3, 3),
-    ("OS", 5, 1, 6),
+    ("OS", 5, 0, 0),
+    ("OS", 5, 0, 1),
     ("T", 5, 0),
     ("R", 2, 2),
     ("R", 2, 3),
@@ -153,7 +155,8 @@ PROGRAM = (
     ("M", 3, 0, 3),
     ("M", 3, 1, 2),
     ("M", 3, 1, 3),
-    ("OS", 6, 0, 6),
+    ("OS", 5, 1, 0),
+    ("OS", 5, 1, 1),
     ("T", 5, 1),
     ("R", 3, 0),
     ("R", 3, 1),
@@ -167,7 +170,8 @@ PROGRAM = (
     ("M", 3, 3, 1),
     ("M", 3, 3, 2),
     ("M", 3, 3, 3),
-    ("OS", 6, 1, 6),
+    ("OS", 6, 0, 0),
+    ("OS", 6, 0, 1),
     ("T", 6, 0),
     ("R", 3, 2),
     ("R", 3, 3),
@@ -181,6 +185,8 @@ PROGRAM = (
     ("M", 4, 0, 3),
     ("M", 4, 1, 2),
     ("M", 4, 1, 3),
+    ("OS", 6, 1, 0),
+    ("OS", 6, 1, 1),
     ("T", 6, 1),
     ("R", 4, 0),
     ("R", 4, 1),
@@ -299,12 +305,12 @@ def tile_rlaattention_pa_kernel(tc, x, freqs_cis, Wqkv, out_0, out_1, out_2):
             nc.scalar.copy(out=ro[:], in_=words.rearrange("r (g p u) -> r g u p", g=2, u=2))
             source[(grp, gp, j)] = (ro[:].rearrange("r g u p -> r (g u p)"), 1)
 
-        def reorder_units(grp, gp, count):
-            words = halves[(grp, gp)][:].bitcast(F32).rearrange("r j w -> r (j w)")[:, 0 : 256 * count]
-            ro = work.tile([P, count, 2, 128], F32, name="rs", bufs=2)
-            nc.scalar.copy(out=ro[:], in_=words.rearrange("r (c p u) -> r c u p", c=count, u=2))
-            for unit in range(count):
-                in_order[(grp, gp, unit)] = ro
+        def reorder_units(grp, gp, gg):
+            words = halves[(grp, gp)][:].bitcast(F32)
+            ro = work.tile([P, 3, 2, 128], F32, name="rs", bufs=2)
+            nc.scalar.copy(out=ro[:], in_=words[:, 0:3, 256 * gg : 256 * (gg + 1)].rearrange("r j (p u) -> r j u p", u=2))
+            for j in range(3):
+                in_order[(grp, gp, 2 * j + gg)] = (ro, j)
 
         def word_columns(entry, gg, u):
             words, step = entry
@@ -345,23 +351,24 @@ def tile_rlaattention_pa_kernel(tc, x, freqs_cis, Wqkv, out_0, out_1, out_2):
                     in_=bank[:].rearrange("p (g u r) -> p g r u", g=2, u=2),
                 )
 
-        def transposes(grp, gp):
-            for gg in range(2):
-                for rp in range(2):
-                    bank = tp_pool.tile([P, 512], F32, name="bank")
-                    for u in range(2):
-                        for jj in range(2):
-                            c0 = 256 * u + 128 * jj
-                            unit = 2 * (2 * rp + jj) + gg
-                            if (grp, gp, unit) in in_order:
-                                columns = in_order[(grp, gp, unit)][:, unit, u, :]
-                            else:
-                                columns = word_columns(source[(grp, gp, 2 * rp + jj)], gg, u)
-                            nc.tensor.transpose(bank[:, c0 : c0 + 128], columns, ident[:])
-                    nc.scalar.copy(
-                        out=pair_tile(grp, gp)[:, gg, 256 * rp : 256 * (rp + 1), :],
-                        in_=bank[:].rearrange("p (u r) -> p r u", u=2),
-                    )
+        def transposes(grp, gp, unsorted_first):
+            banks = ((0, 1), (1, 1), (0, 0), (1, 0)) if unsorted_first else ((0, 0), (0, 1), (1, 0), (1, 1))
+            for gg, rp in banks:
+                bank = tp_pool.tile([P, 512], F32, name="bank")
+                for u in range(2):
+                    for jj in range(2):
+                        c0 = 256 * u + 128 * jj
+                        unit = 2 * (2 * rp + jj) + gg
+                        if (grp, gp, unit) in in_order:
+                            sorted_tile, row_tile = in_order[(grp, gp, unit)]
+                            columns = sorted_tile[:, row_tile, u, :]
+                        else:
+                            columns = word_columns(source[(grp, gp, 2 * rp + jj)], gg, u)
+                        nc.tensor.transpose(bank[:, c0 : c0 + 128], columns, ident[:])
+                nc.scalar.copy(
+                    out=pair_tile(grp, gp)[:, gg, 256 * rp : 256 * (rp + 1), :],
+                    in_=bank[:].rearrange("p (u r) -> p r u", u=2),
+                )
 
         def quantize_x(m):
             c = const.tile([P, PASSES, P], U32, name="xc%d" % m, align_bytes=64)
@@ -474,7 +481,7 @@ def tile_rlaattention_pa_kernel(tc, x, freqs_cis, Wqkv, out_0, out_1, out_2):
             elif kind == "TJ":
                 transposes_row_tile(step[1], step[2])
             elif kind == "T":
-                transposes(step[1], step[2])
+                transposes(step[1], step[2], len(step) > 3)
             elif kind == "QX":
                 quantize_x(step[1])
             elif kind == "Q":

@@ -371,8 +371,8 @@ def tile_rlaattention_pa_kernel(tc, x, freqs_cis, Wqkv, out_0, out_1, out_2):
                 )
 
         def quantize_x(m):
-            c = const.tile([P, PASSES, P], U32, name="xc%d" % m, align_bytes=64)
-            s = const.tile([P, PASSES, P], U8, name="xs%d" % m, align_bytes=64)
+            c = const.tile([P, PASSES, P], U32, name="xc%d" % m, align_bytes=256)
+            s = const.tile([P, PASSES, P], U8, name="xs%d" % m, align_bytes=256)
             nc.vector.quantize_mx(
                 out=c[:].rearrange("p g r -> p (g r)").bitcast(E5X4),
                 scales=s[:].rearrange("p g r -> p (g r)"),
@@ -382,8 +382,8 @@ def tile_rlaattention_pa_kernel(tc, x, freqs_cis, Wqkv, out_0, out_1, out_2):
             scales[("x", m)] = s
 
         def quantize(grp, gp):
-            c = code_pool.tile([P, 2, 512], U32, name="wc", align_bytes=64)
-            s = code_pool.tile([P, 2, 512], U8, name="ws", align_bytes=64)
+            c = code_pool.tile([P, 2, 512], U32, name="wc", align_bytes=256)
+            s = code_pool.tile([P, 2, 512], U8, name="ws", align_bytes=256)
             nc.vector.quantize_mx(
                 out=c[:].rearrange("p g r -> p (g r)").bitcast(E5X4),
                 scales=s[:].rearrange("p g r -> p (g r)"),

@@ -436,14 +436,29 @@ def tile_rlaattention_pa_kernel(tc, x, freqs_cis, Wqkv, out_0, out_1, out_2):
         def rope_add(n, mp, on_vector):
             m12 = prod[(n, mp)]
             eng = nc.vector if on_vector else nc.gpsimd
-            res[(n, mp)] = work.tile([P, 4, 2, HD], F32, name="res", bufs=3)
-            eng.tensor_tensor(
-                out=res[(n, mp)][:].rearrange("p h b d -> p (h b d)"),
-                in0=m12[:, 0].rearrange("p h b d -> p (h b d)"),
-                in1=m12[:, 1].rearrange("p h b d -> p (h b d)"),
-                op=ADD,
-            )
-            store_pair(nc.sync, n, mp)
+            if n == 4:
+                res[(n, mp)] = work.tile([P, 4, 2, HD], F32, name="res", bufs=2)
+                eng.tensor_tensor(
+                    out=res[(n, mp)][:].rearrange("p h b d -> p (h b d)"),
+                    in0=m12[:, 0].rearrange("p h b d -> p (h b d)"),
+                    in1=m12[:, 1].rearrange("p h b d -> p (h b d)"),
+                    op=ADD,
+                )
+                store_pair(nc.sync, n, mp)
+            else:
+                if mp == 0:
+                    res[n] = work.tile([P, 4, 4, HD], F32, name="resg", bufs=2)
+                eng.tensor_tensor(
+                    out=res[n][:, :, 2 * mp : 2 * mp + 2, :].rearrange("p h b d -> p h (b d)"),
+                    in0=m12[:, 0].rearrange("p h b d -> p h (b d)"),
+                    in1=m12[:, 1].rearrange("p h b d -> p h (b d)"),
+                    op=ADD,
+                )
+                if mp == 1:
+                    nc.sync.dma_start(
+                        out=out_rows(n).rearrange("h (p m) d -> p h (m d)", m=4),
+                        in_=res[n][:].rearrange("p h m d -> p h (m d)"),
+                    )
 
         def plain_copy(n, m, alone):
             a3 = acc[(n, m)][:].rearrange("p (h c) -> p h c", h=4)
@@ -453,7 +468,7 @@ def tile_rlaattention_pa_kernel(tc, x, freqs_cis, Wqkv, out_0, out_1, out_2):
                 nc.scalar.dma_start(out=out_rows(n).rearrange("h (p m) d -> p m h d", m=4)[:, m], in_=t[:])
             else:
                 if m % 2 == 0:
-                    res[(n, m // 2)] = work.tile([P, 4, 2, HD], F32, name="res", bufs=3)
+                    res[(n, m // 2)] = work.tile([P, 4, 2, HD], F32, name="res", bufs=2)
                 nc.scalar.copy(out=res[(n, m // 2)][:, :, m % 2, :], in_=a3)
                 if m % 2 == 1:
                     store_pair(nc.scalar, n, m // 2)

@@ -306,10 +306,11 @@ def tile_rlaattention_pa_kernel(tc, x, freqs_cis, Wqkv, out_0, out_1, out_2):
             source[(grp, gp, j)] = (ro[:].rearrange("r g u p -> r (g u p)"), 1)
 
         def reorder_units(grp, gp, gg):
+            count = 3 if gg == 0 else 2
             words = halves[(grp, gp)][:].bitcast(F32)
-            ro = work.tile([P, 3, 2, 128], F32, name="rs", bufs=2)
-            nc.scalar.copy(out=ro[:], in_=words[:, 0:3, 256 * gg : 256 * (gg + 1)].rearrange("r j (p u) -> r j u p", u=2))
-            for j in range(3):
+            ro = work.tile([P, count, 2, 128], F32, name="rs", bufs=2)
+            nc.scalar.copy(out=ro[:], in_=words[:, 0:count, 256 * gg : 256 * (gg + 1)].rearrange("r j (p u) -> r j u p", u=2))
+            for j in range(count):
                 in_order[(grp, gp, 2 * j + gg)] = (ro, j)
 
         def word_columns(entry, gg, u):

from contextlib import ExitStack

import concourse.mybir as mybir
from concourse.masks import make_identity

F32 = mybir.dt.float32
BF16 = mybir.dt.bfloat16
U32 = mybir.dt.uint32
U8 = mybir.dt.uint8
E5X4 = mybir.dt.float8_e5m2_x4
MULT = mybir.AluOpType.mult
ADD = mybir.AluOpType.add

P = 128
HD = 128
K_PASS = 512
PASSES = 4
FLOPS = 2 * 512 * 2048 * 3072

PROGRAM = (
    ("LX", 0),
    ("LJ", 1, 0),
    ("LJ", 1, 1),
    ("LJ", 1, 2),
    ("LJ", 1, 3),
    ("LX", 1),
    ("LF", 0),
    ("LX", 2),
    ("LX", 3),
    ("L", 2, 0),
    ("L", 2, 1),
    ("L", 3, 0),
    ("L", 3, 1),
    ("L", 4, 0),
    ("L", 4, 1),
    ("W", 6),
    ("TX", 0),
    ("W", 1),
    ("QX", 0),
    ("TJ", 1, 0),
    ("W", 1),
    ("TJ", 1, 1),
    ("W", 1),
    ("TJ", 1, 2),
    ("W", 1),
    ("TJ", 1, 3),
    ("W", 1),
    ("Q", 1, 0),
    ("Q", 1, 1),
    ("TX", 1),
    ("TX", 2),
    ("QX", 1),
    ("B", 0),
    ("QX", 2),
    ("M", 0, 0, 0),
    ("M", 0, 0, 1),
    ("M", 0, 0, 2),
    ("M", 0, 0, 3),
    ("TX", 3),
    ("R", 0, 0),
    ("QX", 3),
    ("M", 0, 1, 0),
    ("M", 0, 1, 1),
    ("M", 0, 1, 2),
    ("M", 0, 1, 3),
    ("T", 2, 0),
    ("R", 0, 1),
    ("Q", 2, 0),
    ("A", 0, 0),
    ("L", 5, 0),
    ("M", 0, 2, 0),
    ("M", 0, 2, 1),
    ("M", 0, 2, 2),
    ("M", 0, 2, 3),
    ("T", 2, 1),
    ("R", 0, 2),
    ("Q", 2, 1),
    ("M", 0, 3, 0),
    ("M", 0, 3, 1),
    ("M", 0, 3, 2),
    ("M", 0, 3, 3),
    ("O", 3, 0, 0),
    ("O", 3, 0, 1),
    ("T", 3, 0, 1),
    ("R", 0, 3),
    ("A", 0, 1),
    ("L", 5, 1),
    ("M", 1, 0, 0),
    ("M", 1, 0, 1),
    ("M", 1, 1, 0),
    ("M", 1, 1, 1),
    ("M", 1, 0, 2),
    ("M", 1, 0, 3),
    ("M", 1, 1, 2),
    ("M", 1, 1, 3),
    ("O", 3, 1, 0),
    ("O", 3, 1, 1),
    ("T", 3, 1),
    ("R", 1, 0),
    ("R", 1, 1),
    ("Q", 3, 0),
    ("A", 1, 0),
    ("L", 6, 0),
    ("M", 1, 2, 0),
    ("M", 1, 2, 1),
    ("M", 1, 2, 2),
    ("M", 1, 2, 3),
    ("M", 1, 3, 0),
    ("M", 1, 3, 1),
    ("M", 1, 3, 2),
    ("M", 1, 3, 3),
    ("OS", 4, 0, 0),
    ("OS", 4, 0, 1),
    ("T", 4, 0),
    ("R", 1, 2),
    ("R", 1, 3),
    ("Q", 3, 1),
    ("A", 1, 1),
    ("L", 6, 1),
    ("M", 2, 0, 0),
    ("M", 2, 0, 1),
    ("M", 2, 1, 0),
    ("M", 2, 1, 1),
    ("M", 2, 0, 2),
    ("M", 2, 0, 3),
    ("M", 2, 1, 2),
    ("M", 2, 1, 3),
    ("OS", 4, 1, 0),
    ("OS", 4, 1, 1),
    ("T", 4, 1),
    ("R", 2, 0),
    ("R", 2, 1),
    ("Q", 4, 0),
    ("A", 2, 0),
    ("M", 2, 2, 0),
    ("M", 2, 2, 1),
    ("M", 2, 2, 2),
    ("M", 2, 2, 3),
    ("M", 2, 3, 0),
    ("M", 2, 3, 1),
    ("M", 2, 3, 2),
    ("M", 2, 3, 3),
    ("OS", 5, 0, 0),
    ("OS", 5, 0, 1),
    ("T", 5, 0),
    ("R", 2, 2),
    ("R", 2, 3),
    ("Q", 4, 1),
    ("A", 2, 1),
    ("M", 3, 0, 0),
    ("M", 3, 0, 1),
    ("M", 3, 1, 0),
    ("M", 3, 1, 1),
    ("M", 3, 0, 2),
    ("M", 3, 0, 3),
    ("M", 3, 1, 2),
    ("M", 3, 1, 3),
    ("OS", 5, 1, 0),
    ("OS", 5, 1, 1),
    ("T", 5, 1),
    ("R", 3, 0),
    ("R", 3, 1),
    ("Q", 5, 0),
    ("A", 3, 0),
    ("M", 3, 2, 0),
    ("M", 3, 2, 1),
    ("M", 3, 2, 2),
    ("M", 3, 2, 3),
    ("M", 3, 3, 0),
    ("M", 3, 3, 1),
    ("M", 3, 3, 2),
    ("M", 3, 3, 3),
    ("OS", 6, 0, 0),
    ("OS", 6, 0, 1),
    ("T", 6, 0),
    ("R", 3, 2),
    ("R", 3, 3),
    ("Q", 5, 1),
    ("A", 3, 1),
    ("M", 4, 0, 0),
    ("M", 4, 0, 1),
    ("M", 4, 1, 0),
    ("M", 4, 1, 1),
    ("M", 4, 0, 2),
    ("M", 4, 0, 3),
    ("M", 4, 1, 2),
    ("M", 4, 1, 3),
    ("OS", 6, 1, 0),
    ("OS", 6, 1, 1),
    ("T", 6, 1),
    ("R", 4, 0),
    ("R", 4, 1),
    ("Q", 6, 0),
    ("Q", 6, 1),
    ("A", 4, 0, 1),
    ("M", 4, 2, 0),
    ("M", 4, 2, 1),
    ("M", 4, 2, 2),
    ("M", 4, 2, 3),
    ("M", 4, 3, 0),
    ("M", 4, 3, 1),
    ("M", 4, 3, 2),
    ("M", 4, 3, 3),
    ("R", 4, 2),
    ("R", 4, 3),
    ("A", 4, 1, 1),
    ("M", 5, 0, 0),
    ("M", 5, 0, 1),
    ("M", 5, 0, 2),
    ("M", 5, 0, 3),
    ("M", 5, 1, 0),
    ("M", 5, 1, 1),
    ("M", 5, 1, 2),
    ("M", 5, 1, 3),
    ("C", 5, 0, 1),
    ("C", 5, 1, 1),
    ("M", 5, 2, 0),
    ("M", 5, 2, 1),
    ("M", 5, 2, 2),
    ("M", 5, 2, 3),
    ("M", 5, 3, 0),
    ("M", 5, 3, 1),
    ("M", 5, 3, 2),
    ("M", 5, 3, 3),
    ("C", 5, 2, 1),
    ("C", 5, 3, 1),
)


def tile_rlaattention_pa_kernel(tc, x, freqs_cis, Wqkv, out_0, out_1, out_2):
    nc = tc.nc
    with ExitStack() as ctx:
        const = ctx.enter_context(tc.tile_pool(name="const", bufs=1))
        raw = ctx.enter_context(tc.tile_pool(name="raw", bufs=6))
        grp_pool = ctx.enter_context(tc.tile_pool(name="grp", bufs=3))
        code_pool = ctx.enter_context(tc.tile_pool(name="code", bufs=8))
        work = ctx.enter_context(tc.tile_pool(name="work", bufs=2))
        tp_pool = ctx.enter_context(tc.psum_pool(name="tp", bufs=4))
        acc_pool = ctx.enter_context(tc.psum_pool(name="acc", bufs=4))
        ctx.enter_context(tc.manual_schedule())

        x_view = x.flatten_outer_dims().rearrange("(p m) k -> p m k", m=4)
        source = {}
        grouped = {}
        codes = {}
        scales = {}
        acc = {}
        prod = {}
        res = {}
        idle = {}
        halves = {}
        in_order = {}

        f_sb = const.tile([P, 4, HD], BF16, name="f_sb")
        ident = const.tile([P, P], F32, name="ident")
        make_identity(nc, ident[:])
        warm = const.tile([P, 1], F32, name="warm")
        nc.scalar.copy(out=warm[:], in_=ident[:, 0:1])
        zeros = const.tile([P, 512], BF16, name="zeros")
        nc.vector.memset(zeros[:], 0.0)
        tab = const.tile([P, 2, 4, HD], F32, name="tab")

        def w_rows(grp):
            return Wqkv[(grp - 1) * 512 : grp * 512, :].rearrange("(j p) k -> p j k", p=P)

        def load_f():
            nc.sync.dma_start(out=f_sb[:], in_=freqs_cis.rearrange("(p m) d -> p m d", m=4))

        def load_x(m):
            t = const.tile([P, K_PASS * PASSES], BF16, name="rawx%d" % m)
            nc.sync.dma_start(out=t[:], in_=x_view[:, m, :])
            source[("x", m)] = t

        def load_row_tile(grp, j):
            t = const.tile([P, K_PASS * PASSES], BF16, name="rawj%d" % j)
            nc.sync.dma_start(out=t[:], in_=w_rows(grp)[:, j, :])
            for gp in range(2):
                source[(grp, gp, j)] = (t[:].bitcast(F32)[:, 512 * gp : 512 * (gp + 1)], 2)

        def load_half(grp, gp):
            t = raw.tile([P, 4, 2 * K_PASS], BF16, name="rawk")
            nc.sync.dma_start(out=t[:], in_=w_rows(grp)[:, :, 2 * K_PASS * gp : 2 * K_PASS * (gp + 1)])
            halves[(grp, gp)] = t
            for j in range(4):
                source[(grp, gp, j)] = (t[:, j, :].bitcast(F32), 2)

        def keep_warm(count):
            if len(idle) == 0:
                idle[0] = acc_pool.tile([P, 512], F32, name="acc")
            for i in range(count):
                nc.tensor.matmul(out=idle[0][:], lhsT=zeros[:, 0:P], rhs=zeros[:], start=True, stop=True)

        def build_tables():
            f_pairs = f_sb[:].rearrange("p m (j e) -> p m j e", e=2)
            a_pairs = tab[:, 0].rearrange("p m (j e) -> p m j e", e=2)
            b_pairs = tab[:, 1].rearrange("p m (j e) -> p m j e", e=2)
            nc.vector.tensor_copy(out=a_pairs[:, :, :, 0], in_=f_pairs[:, :, :, 1])
            nc.vector.tensor_copy(out=a_pairs[:, :, :, 1], in_=f_pairs[:, :, :, 1])
            nc.vector.tensor_copy(out=b_pairs[:, :, :, 1], in_=f_pairs[:, :, :, 0])
            nc.vector.tensor_scalar_mul(out=b_pairs[:, :, :, 0], in0=f_pairs[:, :, :, 0], scalar1=-1.0)

        def reorder(grp, gp, j):
            words, step = source[(grp, gp, j)]
            ro = work.tile([P, 2, 2, 128], F32, name="ro", bufs=4)
            nc.scalar.copy(out=ro[:], in_=words.rearrange("r (g p u) -> r g u p", g=2, u=2))
            source[(grp, gp, j)] = (ro[:].rearrange("r g u p -> r (g u p)"), 1)

        def reorder_units(grp, gp, gg):
            count = 3 if gg == 0 else 2
            words = halves[(grp, gp)][:].bitcast(F32)
            ro = work.tile([P, count, 2, 128], F32, name="rs", bufs=2)
            nc.scalar.copy(out=ro[:], in_=words[:, 0:count, 256 * gg : 256 * (gg + 1)].rearrange("r j (p u) -> r j u p", u=2))
            for j in range(count):
                in_order[(grp, gp, 2 * j + gg)] = (ro, j)

        def word_columns(entry, gg, u):
            words, step = entry
            if step == 2:
                return words[:, 256 * gg + u : 256 * (gg + 1) : 2]
            return words[:, 256 * gg + 128 * u : 256 * gg + 128 * (u + 1)]

        def pair_tile(grp, gp):
            if (grp, gp) not in grouped:
                grouped[(grp, gp)] = grp_pool.tile([P, 2 * 4 * 512], BF16, name="gt", align_bytes=64)
            return grouped[(grp, gp)][:].bitcast(F32).rearrange("p (g r u) -> p g r u", g=2, u=2)

        def transposes_x(m):
            words = (source[("x", m)][:].bitcast(F32), 2)
            gt = grp_pool.tile([P, 4 * 512], BF16, name="gx", align_bytes=64, bufs=2)
            gw = gt[:].bitcast(F32).rearrange("p (g r u) -> p g r u", g=PASSES, u=2)
            for gp in range(2):
                bank = tp_pool.tile([P, 512], F32, name="bank")
                for gg in range(2):
                    for u in range(2):
                        c0 = 256 * gg + 128 * u
                        nc.tensor.transpose(bank[:, c0 : c0 + 128], word_columns(words, 2 * gp + gg, u), ident[:])
                nc.scalar.copy(
                    out=gw[:, 2 * gp : 2 * gp + 2, :, :],
                    in_=bank[:].rearrange("p (g u r) -> p g r u", g=2, u=2),
                )
            grouped[("x", m)] = gt

        def transposes_row_tile(grp, j):
            for gp in range(2):
                bank = tp_pool.tile([P, 512], F32, name="bank")
                for gg in range(2):
                    for u in range(2):
                        c0 = 256 * gg + 128 * u
                        nc.tensor.transpose(bank[:, c0 : c0 + 128], word_columns(source[(grp, gp, j)], gg, u), ident[:])
                nc.scalar.copy(
                    out=pair_tile(grp, gp)[:, :, 128 * j : 128 * (j + 1), :],
                    in_=bank[:].rearrange("p (g u r) -> p g r u", g=2, u=2),
                )

        def transposes(grp, gp, unsorted_first):
            banks = ((0, 1), (1, 1), (0, 0), (1, 0)) if unsorted_first else ((0, 0), (0, 1), (1, 0), (1, 1))
            for gg, rp in banks:
                bank = tp_pool.tile([P, 512], F32, name="bank")
                for u in range(2):
                    for jj in range(2):
                        c0 = 256 * u + 128 * jj
                        unit = 2 * (2 * rp + jj) + gg
                        if (grp, gp, unit) in in_order:
                            sorted_tile, row_tile = in_order[(grp, gp, unit)]
                            columns = sorted_tile[:, row_tile, u, :]
                        else:
                            columns = word_columns(source[(grp, gp, 2 * rp + jj)], gg, u)
                        nc.tensor.transpose(bank[:, c0 : c0 + 128], columns, ident[:])
                nc.scalar.copy(
                    out=pair_tile(grp, gp)[:, gg, 256 * rp : 256 * (rp + 1), :],
                    in_=bank[:].rearrange("p (u r) -> p r u", u=2),
                )

        def quantize_x(m):
            c = const.tile([P, PASSES, P], U32, name="xc%d" % m, align_bytes=256)
            s = const.tile([P, PASSES, P], U8, name="xs%d" % m, align_bytes=256)
            nc.vector.quantize_mx(
                out=c[:].rearrange("p g r -> p (g r)").bitcast(E5X4),
                scales=s[:].rearrange("p g r -> p (g r)"),
                in_=grouped[("x", m)][:],
            )
            codes[("x", m)] = c
            scales[("x", m)] = s

        def quantize(grp, gp):
            c = code_pool.tile([P, 2, 512], U32, name="wc", align_bytes=256)
            s = code_pool.tile([P, 2, 512], U8, name="ws", align_bytes=256)
            nc.vector.quantize_mx(
                out=c[:].rearrange("p g r -> p (g r)").bitcast(E5X4),
                scales=s[:].rearrange("p g r -> p (g r)"),
                in_=grouped[(grp, gp)][:],
            )
            codes[(grp, gp)] = c
            scales[(grp, gp)] = s

        def mx(n, m, g):
            if g == 0:
                acc[(n, m)] = acc_pool.tile([P, 512], F32, name="acc")
            nc.tensor.matmul_mx(
                out=acc[(n, m)][:],
                lhsT=codes[("x", m)][:, g, :].bitcast(E5X4),
                lhsT_scale=scales[("x", m)][:, g, :],
                rhs=codes[(n + 1, g // 2)][:, g % 2, :].bitcast(E5X4),
                rhs_scale=scales[(n + 1, g // 2)][:, g % 2, :],
                start=(g == 0),
                stop=(g == PASSES - 1),
            )

        def rope_products(n, m):
            if m % 2 == 0:
                prod[(n, m // 2)] = work.tile([P, 2, 4, 2, HD], F32, name="m12")
            m12 = prod[(n, m // 2)]
            nc.vector.tensor_tensor(
                out=m12[:, 0, :, m % 2, :],
                in0=acc[(n, m)][:].rearrange("p (h c) -> p h c", h=4),
                in1=tab[:, 0, m : m + 1, :].to_broadcast([P, 4, HD]),
                op=MULT,
            )
            nc.vector.tensor_tensor(
                out=m12[:, 1, :, m % 2, :].rearrange("p h (j e) -> p h j e", e=2),
                in0=acc[(n, m)][:].rearrange("p (h j e) -> p h j e", h=4, e=2)[:, :, :, ::-1],
                in1=tab[:, 1, m : m + 1, :].rearrange("p o (j e) -> p o j e", e=2).to_broadcast([P, 4, HD // 2, 2]),
                op=MULT,
            )

        def out_rows(n):
            if n < 4:
                return out_0[0, 4 * n : 4 * n + 4]
            if n == 4:
                return out_1[0]
            return out_2[0]

        def store_pair(queue, n, mp):
            view = out_rows(n).rearrange("h (p a b) d -> p a h (b d)", a=2, b=2)
            queue.dma_start(out=view[:, mp], in_=res[(n, mp)][:].rearrange("p h b d -> p h (b d)"))

        def rope_add(n, mp, on_vector):
            m12 = prod[(n, mp)]
            eng = nc.vector if on_vector else nc.gpsimd
            if n == 4:
                res[(n, mp)] = work.tile([P, 4, 2, HD], F32, name="res", bufs=2)
                eng.tensor_tensor(
                    out=res[(n, mp)][:].rearrange("p h b d -> p (h b d)"),
                    in0=m12[:, 0].rearrange("p h b d -> p (h b d)"),
                    in1=m12[:, 1].rearrange("p h b d -> p (h b d)"),
                    op=ADD,
                )
                store_pair(nc.sync, n, mp)
            else:
                if mp == 0:
                    res[n] = work.tile([P, 4, 4, HD], F32, name="resg", bufs=2)
                eng.tensor_tensor(
                    out=res[n][:, :, 2 * mp : 2 * mp + 2, :].rearrange("p h b d -> p h (b d)"),
                    in0=m12[:, 0].rearrange("p h b d -> p h (b d)"),
                    in1=m12[:, 1].rearrange("p h b d -> p h (b d)"),
                    op=ADD,
                )
                if mp == 1:
                    nc.sync.dma_start(
                        out=out_rows(n).rearrange("h (p m) d -> p h (m d)", m=4),
                        in_=res[n][:].rearrange("p h m d -> p h (m d)"),
                    )

        def plain_copy(n, m, alone):
            a3 = acc[(n, m)][:].rearrange("p (h c) -> p h c", h=4)
            if alone:
                t = work.tile([P, 4, HD], F32, name="res1", bufs=4)
                nc.scalar.copy(out=t[:], in_=a3)
                nc.scalar.dma_start(out=out_rows(n).rearrange("h (p m) d -> p m h d", m=4)[:, m], in_=t[:])
            else:
                if m % 2 == 0:
                    res[(n, m // 2)] = work.tile([P, 4, 2, HD], F32, name="res", bufs=2)
                nc.scalar.copy(out=res[(n, m // 2)][:, :, m % 2, :], in_=a3)
                if m % 2 == 1:
                    store_pair(nc.scalar, n, m // 2)

        for step in PROGRAM:
            kind = step[0]
            if kind == "LX":
                load_x(step[1])
            elif kind == "LF":
                load_f()
            elif kind == "LJ":
                load_row_tile(step[1], step[2])
            elif kind == "L":
                load_half(step[1], step[2])
            elif kind == "W":
                keep_warm(step[1])
            elif kind == "B":
                build_tables()
            elif kind == "O":
                reorder(step[1], step[2], step[3])
            elif kind == "OS":
                reorder_units(step[1], step[2], step[3])
            elif kind == "TX":
                transposes_x(step[1])
            elif kind == "TJ":
                transposes_row_tile(step[1], step[2])
            elif kind == "T":
                transposes(step[1], step[2], len(step) > 3)
            elif kind == "QX":
                quantize_x(step[1])
            elif kind == "Q":
                quantize(step[1], step[2])
            elif kind == "M":
                mx(step[1], step[2], step[3])
            elif kind == "R":
                rope_products(step[1], step[2])
            elif kind == "A":
                rope_add(step[1], step[2], len(step) > 3)
            elif kind == "C":
                plain_copy(step[1], step[2], step[3] == 1)
